import numpy as np
import ml_dtypes


def mxq(x, axis, fmt="e4m3"):
    dtype, down = {"e4m3": (ml_dtypes.float8_e4m3fn, 7), "e5m2": (ml_dtypes.float8_e5m2, 14)}[fmt]
    v = np.moveaxis(np.asarray(x, np.float32).astype(ml_dtypes.bfloat16).astype(np.float64), axis, -1)
    blocks = v.reshape(v.shape[:-1] + (-1, 32))
    amax = np.abs(blocks).max(-1, keepdims=True)
    byte = np.maximum(np.where(amax > 0, np.frexp(amax)[1] - 1 + 127, 0) - down, 1)
    scale = np.exp2(byte - 127.0)
    codes = (blocks / scale).astype(np.float32).astype(dtype).astype(np.float64)
    return np.moveaxis((codes * scale).reshape(v.shape), -1, axis)


WIDE = False


def mx_kscale(k, group=512):
    if not WIDE:
        return np.ones(k)
    levels = np.array([10, -10, 5, -5, 0])
    if group != 512:
        return np.exp2(np.random.permutation(np.resize(levels, k // group))).repeat(group)
    a = np.random.permutation(np.resize(levels, k // 512 * 4)).reshape(k // 512, 4)
    idx = np.arange(k)
    return np.exp2(a[idx // 512, idx % 128 // 32])


BF16 = ml_dtypes.bfloat16


def bf(x):
    return np.asarray(x, np.float32).astype(BF16)


def f64(x):
    return np.asarray(x).astype(np.float64)


B, IN, OUT = 1024, 2048, 2048
QI, QO = IN // 4, OUT // 4


def _hamilton_weight(Wr, Wi, Wj, Wk):
    return np.concatenate([
        np.concatenate([Wr, Wi, Wj, Wk], axis=1),
        np.concatenate([-Wi, Wr, Wk, -Wj], axis=1),
        np.concatenate([-Wj, -Wk, Wr, Wi], axis=1),
        np.concatenate([-Wk, Wj, -Wi, Wr], axis=1),
    ], axis=0)


def _hamilton_bias(br, bi, bj, bk):
    return np.concatenate([
        br - bi - bj - bk,
        br + bi + bj - bk,
        br - bi + bj + bk,
        br + bi - bj + bk,
    ], axis=0)


def setup_inputs():
    s = mx_kscale(QI, group=QI // 4)
    c = 1.0 / np.sqrt(QI)
    return {"x": bf(np.random.standard_normal((B, IN)) * np.tile(s, 4)),
            "Wr": bf(np.random.standard_normal((QI, QO)) * c / s[:, None]),
            "Wi": bf(np.random.standard_normal((QI, QO)) * c / s[:, None]),
            "Wj": bf(np.random.standard_normal((QI, QO)) * c / s[:, None]),
            "Wk": bf(np.random.standard_normal((QI, QO)) * c / s[:, None]),
            "br": bf(np.random.standard_normal(QO) * 0.3),
            "bi": bf(np.random.standard_normal(QO) * 0.3),
            "bj": bf(np.random.standard_normal(QO) * 0.3),
            "bk": bf(np.random.standard_normal(QO) * 0.3)}


def reference(x, Wr, Wi, Wj, Wk, br, bi, bj, bk):
    Wq = mxq(np.concatenate([f64(Wr), f64(Wi), f64(Wj), f64(Wk)], axis=0), 0, "e4m3")
    W = _hamilton_weight(Wq[:QI], Wq[QI:2 * QI], Wq[2 * QI:3 * QI], Wq[3 * QI:])
    b = _hamilton_bias(f64(br), f64(bi), f64(bj), f64(bk))
    return (mxq(f64(x), 1, "e4m3") @ W) + b

@@ -1,0 +1,192 @@
+from contextlib import ExitStack
+
+import concourse.mybir as mybir
+from concourse.masks import make_identity
+
+F32 = mybir.dt.float32
+BF16 = mybir.dt.bfloat16
+U32 = mybir.dt.uint32
+U8 = mybir.dt.uint8
+FP8X4 = mybir.dt.float8_e4m3fn_x4
+
+P = 128
+PACK = 4
+B, IN, OUT = 1024, 2048, 2048
+Q = 512
+CHUNKS = 4
+ROW_TILES = B // P
+FLOPS = 2 * B * IN * OUT
+
+HAMILTON = (
+    ((0, 1), (1, 1), (2, 1), (3, 1)),
+    ((1, -1), (0, 1), (3, 1), (2, -1)),
+    ((2, -1), (3, -1), (0, 1), (1, 1)),
+    ((3, -1), (2, 1), (1, -1), (0, 1)),
+)
+OPERANDS = ((0, 1), (1, 1), (2, 1), (3, 1), (1, -1), (2, -1), (3, -1))
+BIAS_SIGN = (
+    (1, -1, -1, -1),
+    (1, 1, 1, -1),
+    (1, -1, 1, 1),
+    (1, 1, -1, 1),
+)
+
+
+def tile_quaternionlinear_kernel(tc, x, Wr, Wi, Wj, Wk, br, bi, bj, bk, out):
+    nc = tc.nc
+    weights = (Wr, Wi, Wj, Wk)
+    biases = (br, bi, bj, bk)
+
+    with ExitStack() as ctx:
+        keep = ctx.enter_context(tc.tile_pool(name="keep", bufs=1))
+        x_stage = ctx.enter_context(tc.tile_pool(name="x_stage", bufs=4))
+        w_stage = ctx.enter_context(tc.tile_pool(name="w_stage", bufs=2))
+        out_stage = ctx.enter_context(tc.tile_pool(name="out_stage", bufs=6))
+        flip_banks = ctx.enter_context(tc.psum_pool(name="flip_banks", bufs=4))
+        sum_banks = ctx.enter_context(tc.psum_pool(name="sum_banks", bufs=4))
+
+        ctx.enter_context(tc.manual_schedule())
+
+        identity = keep.tile([P, P], F32)
+        bias_rows = keep.tile([P, Q], BF16)
+        bias_signs = keep.tile([P, CHUNKS, P], BF16)
+        bias_all = keep.tile([P, CHUNKS, Q], F32)
+        x_rows = keep.tile([P, ROW_TILES, IN], BF16)
+        x_codes = keep.tile([P, ROW_TILES, CHUNKS * P], U32, align_bytes=64)
+        x_scales = keep.tile([P, ROW_TILES, CHUNKS * P], U8, align_bytes=64)
+        w_rows = keep.tile([P, CHUNKS, PACK, Q], BF16)
+        w_grouped = keep.tile([P, CHUNKS, Q, PACK], BF16, align_bytes=64)
+        w_codes = keep.tile([P, 2, CHUNKS, Q], U32, align_bytes=64)
+        w_scales = keep.tile([P, 2, CHUNKS, Q], U8, align_bytes=64)
+
+        make_identity(nc, identity[:])
+        nc.vector.memset(bias_rows[:], 0.0)
+        for c in range(CHUNKS):
+            for v in range(4):
+                nc.vector.memset(bias_signs[32 * v : 32 * v + 32, c, :], float(BIAS_SIGN[c][v]))
+
+        for v in range(4):
+            nc.scalar.dma_start(
+                out=bias_rows[32 * v : 32 * v + 1, :], in_=biases[v].rearrange("(o n) -> o n", o=1)
+            )
+
+        def load_weight(q):
+            nc.sync.dma_start(
+                out=w_rows[:, q, :, :], in_=weights[q].rearrange("(p t) n -> p t n", t=PACK)
+            )
+
+        def load_x(m):
+            nc.sync.dma_start(out=x_rows[:, m, :], in_=x[m * P : (m + 1) * P, :])
+
+        load_x(0)
+        for q in range(CHUNKS):
+            load_weight(q)
+        for m in range(1, ROW_TILES):
+            load_x(m)
+
+        def combine_bias():
+            for c in range(CHUNKS):
+                bias_sum = flip_banks.tile([P, Q], F32, name="bias_sum", tag="flipped")
+                nc.tensor.matmul(
+                    out=bias_sum[:], lhsT=bias_signs[:, c, :], rhs=bias_rows[:], start=True, stop=True
+                )
+                nc.scalar.copy(out=bias_all[:, c, :], in_=bias_sum[:])
+
+        def lay_out(q, sign):
+            plain = w_grouped[:, q, :, :].rearrange("p n t -> p (n t)")
+            if sign < 0:
+                negated = w_stage.tile([P, Q * PACK], BF16, align_bytes=64)
+                nc.vector.tensor_scalar_mul(out=negated[:], in0=plain, scalar1=-1.0)
+                return negated[:]
+            half = Q // 2
+            for copy, cols in ((nc.vector.tensor_copy, slice(0, half)), (nc.scalar.copy, slice(half, Q))):
+                copy(
+                    out=w_grouped[:, q, cols, :].rearrange("p (c i) t -> p c t i", i=4),
+                    in_=w_rows[:, q, :, cols].rearrange("p t (c i) -> p c t i", i=4),
+                )
+            return plain
+
+        def quantise_operand(q, sign, values):
+            s = 0 if sign > 0 else 1
+            nc.vector.quantize_mx(
+                out=w_codes[:, s, q, :].bitcast(FP8X4), scales=w_scales[:, s, q, :], in_=values
+            )
+
+        def transpose_x(m):
+            words = x_rows[:, m, :].bitcast(F32).rearrange("p (g j u) -> p g u j", g=CHUNKS, u=2)
+            grouped = x_stage.tile([P, CHUNKS * P * PACK], BF16, align_bytes=64, name="x_grouped")
+            grouped_words = grouped[:].bitcast(F32).rearrange("p (g r u) -> p g r u", g=CHUNKS, u=2)
+            for h in range(2):
+                flipped = flip_banks.tile([P, 2, 2, P], F32, name="flipped", tag="flipped")
+                for gi in range(2):
+                    for u in range(2):
+                        nc.tensor.transpose(flipped[:, gi, u, :], words[:, 2 * h + gi, u, :], identity[:])
+                nc.scalar.copy(
+                    out=grouped_words[:, 2 * h : 2 * h + 2, :, :],
+                    in_=flipped[:].rearrange("p g u r -> p g r u"),
+                )
+            return grouped
+
+        def quantise_x(m, grouped):
+            nc.vector.quantize_mx(
+                out=x_codes[:, m, :].bitcast(FP8X4), scales=x_scales[:, m, :], in_=grouped[:]
+            )
+
+        def mx_pass(sums, m, g, c, start, stop):
+            q, sign = HAMILTON[g][c]
+            s = 0 if sign > 0 else 1
+            rows = slice(g * P, (g + 1) * P)
+            nc.tensor.matmul_mx(
+                out=sums[:],
+                lhsT=x_codes[:, m, rows].bitcast(FP8X4),
+                lhsT_scale=x_scales[:, m, rows],
+                rhs=w_codes[:, s, q, :].bitcast(FP8X4),
+                rhs_scale=w_scales[:, s, q, :],
+                start=start,
+                stop=stop,
+            )
+
+        def finish(sums, m, c):
+            result = out_stage.tile([P, Q], F32, name="result")
+            nc.vector.tensor_tensor(
+                out=result[:], in0=sums[:], in1=bias_all[:, c, :], op=mybir.AluOpType.add
+            )
+            nc.sync.dma_start(out=out[m * P : (m + 1) * P, c * Q : (c + 1) * Q], in_=result[:])
+
+        LAST_REGROUP = CHUNKS - 2
+        grouped = {0: transpose_x(0)}
+        values = {0: lay_out(*OPERANDS[0])}
+        quantise_x(0, grouped[0])
+        first_sums = [sum_banks.tile([P, Q], F32, name="sums", tag="sums") for c in range(CHUNKS)]
+        passes_done = [0] * CHUNKS
+        closed = []
+        for i, (q, sign) in enumerate(OPERANDS):
+            if i + 1 < len(OPERANDS):
+                values[i + 1] = lay_out(*OPERANDS[i + 1])
+            quantise_operand(q, sign, values[i])
+            for g in range(CHUNKS):
+                for c in range(CHUNKS):
+                    if HAMILTON[g][c] == (q, sign):
+                        passes_done[c] += 1
+                        mx_pass(first_sums[c], 0, g, c, start=(passes_done[c] == 1), stop=(passes_done[c] == CHUNKS))
+                        if passes_done[c] == CHUNKS:
+                            closed.append(c)
+            if i == LAST_REGROUP:
+                combine_bias()
+            if LAST_REGROUP < i < LAST_REGROUP + CHUNKS:
+                grouped[i - LAST_REGROUP] = transpose_x(i - LAST_REGROUP)
+        quantise_x(1, grouped[1])
+        for c in closed:
+            finish(first_sums[c], 0, c)
+
+        for m in range(1, ROW_TILES):
+            if m % 2 == 1 and m + 4 < ROW_TILES:
+                for a in (m + 3, m + 4):
+                    grouped[a] = transpose_x(a)
+            if m + 1 < ROW_TILES:
+                quantise_x(m + 1, grouped[m + 1])
+            for c in range(CHUNKS):
+                sums = sum_banks.tile([P, Q], F32, name="sums", tag="sums")
+                for g in range(CHUNKS):
+                    mx_pass(sums, m, g, c, start=(g == 0), stop=(g == CHUNKS - 1))
+                finish(sums, m, c)

@@ -66,7 +66,7 @@ def tile_quaternionlinear_kernel(tc, x, Wr, Wi, Wj, Wk, br, bi, bj, bk, out):
                 nc.vector.memset(bias_signs[32 * v : 32 * v + 32, c, :], float(BIAS_SIGN[c][v]))
 
         for v in range(4):
-            nc.scalar.dma_start(
+            nc.sync.dma_start(
                 out=bias_rows[32 * v : 32 * v + 1, :], in_=biases[v].rearrange("(o n) -> o n", o=1)
             )
 
@@ -86,11 +86,12 @@ def tile_quaternionlinear_kernel(tc, x, Wr, Wi, Wj, Wk, br, bi, bj, bk, out):
 
         def combine_bias():
             for c in range(CHUNKS):
-                bias_sum = flip_banks.tile([P, Q], F32, name="bias_sum", tag="flipped")
+                bias_sum = sum_banks.tile([P, Q], F32, name="bias_sum", tag="sums")
                 nc.tensor.matmul(
                     out=bias_sum[:], lhsT=bias_signs[:, c, :], rhs=bias_rows[:], start=True, stop=True
                 )
-                nc.scalar.copy(out=bias_all[:, c, :], in_=bias_sum[:])
+                copy = nc.vector.tensor_copy if c % 2 == 0 else nc.scalar.copy
+                copy(out=bias_all[:, c, :], in_=bias_sum[:])
 
         def lay_out(q, sign):
             plain = w_grouped[:, q, :, :].rearrange("p n t -> p (n t)")
@@ -153,17 +154,20 @@ def tile_quaternionlinear_kernel(tc, x, Wr, Wi, Wj, Wk, br, bi, bj, bk, out):
             )
             nc.sync.dma_start(out=out[m * P : (m + 1) * P, c * Q : (c + 1) * Q], in_=result[:])
 
+        combine_bias()
+
         LAST_REGROUP = CHUNKS - 2
-        grouped = {0: transpose_x(0)}
-        values = {0: lay_out(*OPERANDS[0])}
-        quantise_x(0, grouped[0])
+        w_values = {0: lay_out(*OPERANDS[0])}
+        x_values = {0: transpose_x(0)}
         first_sums = [sum_banks.tile([P, Q], F32, name="sums", tag="sums") for c in range(CHUNKS)]
         passes_done = [0] * CHUNKS
         closed = []
         for i, (q, sign) in enumerate(OPERANDS):
             if i + 1 < len(OPERANDS):
-                values[i + 1] = lay_out(*OPERANDS[i + 1])
-            quantise_operand(q, sign, values[i])
+                w_values[i + 1] = lay_out(*OPERANDS[i + 1])
+            quantise_operand(q, sign, w_values[i])
+            if i == 0:
+                quantise_x(0, x_values[0])
             for g in range(CHUNKS):
                 for c in range(CHUNKS):
                     if HAMILTON[g][c] == (q, sign):
@@ -171,20 +175,18 @@ def tile_quaternionlinear_kernel(tc, x, Wr, Wi, Wj, Wk, br, bi, bj, bk, out):
                         mx_pass(first_sums[c], 0, g, c, start=(passes_done[c] == 1), stop=(passes_done[c] == CHUNKS))
                         if passes_done[c] == CHUNKS:
                             closed.append(c)
-            if i == LAST_REGROUP:
-                combine_bias()
-            if LAST_REGROUP < i < LAST_REGROUP + CHUNKS:
-                grouped[i - LAST_REGROUP] = transpose_x(i - LAST_REGROUP)
-        quantise_x(1, grouped[1])
+            if LAST_REGROUP <= i <= LAST_REGROUP + 1:
+                x_values[i - LAST_REGROUP + 1] = transpose_x(i - LAST_REGROUP + 1)
+        quantise_x(1, x_values[1])
         for c in closed:
             finish(first_sums[c], 0, c)
 
         for m in range(1, ROW_TILES):
-            if m % 2 == 1 and m + 4 < ROW_TILES:
-                for a in (m + 3, m + 4):
-                    grouped[a] = transpose_x(a)
+            if m % 2 == 1:
+                for a in range(m + 2, min(m + 4, ROW_TILES)):
+                    x_values[a] = transpose_x(a)
             if m + 1 < ROW_TILES:
-                quantise_x(m + 1, grouped[m + 1])
+                quantise_x(m + 1, x_values[m + 1])
             for c in range(CHUNKS):
                 sums = sum_banks.tile([P, Q], F32, name="sums", tag="sums")
                 for g in range(CHUNKS):

@@ -41,6 +41,7 @@ def tile_quaternionlinear_kernel(tc, x, Wr, Wi, Wj, Wk, br, bi, bj, bk, out):
         keep = ctx.enter_context(tc.tile_pool(name="keep", bufs=1))
         x_stage = ctx.enter_context(tc.tile_pool(name="x_stage", bufs=4))
         w_stage = ctx.enter_context(tc.tile_pool(name="w_stage", bufs=2))
+        sort_stage = ctx.enter_context(tc.tile_pool(name="sort_stage", bufs=4))
         out_stage = ctx.enter_context(tc.tile_pool(name="out_stage", bufs=6))
         flip_banks = ctx.enter_context(tc.psum_pool(name="flip_banks", bufs=4))
         sum_banks = ctx.enter_context(tc.psum_pool(name="sum_banks", bufs=4))
@@ -59,8 +60,8 @@ def tile_quaternionlinear_kernel(tc, x, Wr, Wi, Wj, Wk, br, bi, bj, bk, out):
         w_codes = keep.tile([P, 2, CHUNKS, Q], U32, align_bytes=64)
         w_scales = keep.tile([P, 2, CHUNKS, Q], U8, align_bytes=64)
 
+        nc.gpsimd.memset(bias_rows[:].bitcast(F32), 0.0)
         make_identity(nc, identity[:])
-        nc.vector.memset(bias_rows[:], 0.0)
         for c in range(CHUNKS):
             for v in range(4):
                 nc.vector.memset(bias_signs[32 * v : 32 * v + 32, c, :], float(BIAS_SIGN[c][v]))
@@ -113,8 +114,15 @@ def tile_quaternionlinear_kernel(tc, x, Wr, Wi, Wj, Wk, br, bi, bj, bk, out):
                 out=w_codes[:, s, q, :].bitcast(FP8X4), scales=w_scales[:, s, q, :], in_=values
             )
 
-        def transpose_x(m):
-            words = x_rows[:, m, :].bitcast(F32).rearrange("p (g j u) -> p g u j", g=CHUNKS, u=2)
+        def word_pairs(m):
+            return x_rows[:, m, :].bitcast(F32).rearrange("p (g j u) -> p g u j", g=CHUNKS, u=2)
+
+        def sort_x(m):
+            sorted_words = sort_stage.tile([P, CHUNKS, 2, P], F32)
+            nc.scalar.copy(out=sorted_words[:], in_=word_pairs(m))
+            return sorted_words[:]
+
+        def transpose_x(m, words):
             grouped = x_stage.tile([P, CHUNKS * P * PACK], BF16, align_bytes=64, name="x_grouped")
             grouped_words = grouped[:].bitcast(F32).rearrange("p (g r u) -> p g r u", g=CHUNKS, u=2)
             for h in range(2):
@@ -133,7 +141,8 @@ def tile_quaternionlinear_kernel(tc, x, Wr, Wi, Wj, Wk, br, bi, bj, bk, out):
                 out=x_codes[:, m, :].bitcast(FP8X4), scales=x_scales[:, m, :], in_=grouped[:]
             )
 
-        def mx_pass(sums, m, g, c, start, stop):
+        def mx_pass(sums, m, g, c, first, width, start, stop):
+            cols = slice(first, first + width)
             q, sign = HAMILTON[g][c]
             s = 0 if sign > 0 else 1
             rows = slice(g * P, (g + 1) * P)
@@ -141,24 +150,27 @@ def tile_quaternionlinear_kernel(tc, x, Wr, Wi, Wj, Wk, br, bi, bj, bk, out):
                 out=sums[:],
                 lhsT=x_codes[:, m, rows].bitcast(FP8X4),
                 lhsT_scale=x_scales[:, m, rows],
-                rhs=w_codes[:, s, q, :].bitcast(FP8X4),
-                rhs_scale=w_scales[:, s, q, :],
+                rhs=w_codes[:, s, q, cols].bitcast(FP8X4),
+                rhs_scale=w_scales[:, s, q, cols],
                 start=start,
                 stop=stop,
             )
 
-        def finish(sums, m, c):
-            result = out_stage.tile([P, Q], F32, name="result")
+        def finish(sums, m, c, first, width):
+            result = out_stage.tile([P, width], F32, name="result")
             nc.vector.tensor_tensor(
-                out=result[:], in0=sums[:], in1=bias_all[:, c, :], op=mybir.AluOpType.add
+                out=result[:], in0=sums[:], in1=bias_all[:, c, first : first + width], op=mybir.AluOpType.add
             )
-            nc.sync.dma_start(out=out[m * P : (m + 1) * P, c * Q : (c + 1) * Q], in_=result[:])
+            nc.sync.dma_start(
+                out=out[m * P : (m + 1) * P, c * Q + first : c * Q + first + width], in_=result[:]
+            )
 
         combine_bias()
 
         LAST_REGROUP = CHUNKS - 2
         w_values = {0: lay_out(*OPERANDS[0])}
-        x_values = {0: transpose_x(0)}
+        x_values = {0: transpose_x(0, word_pairs(0))}
+        x_sorted = {}
         first_sums = [sum_banks.tile([P, Q], F32, name="sums", tag="sums") for c in range(CHUNKS)]
         passes_done = [0] * CHUNKS
         closed = []
@@ -172,23 +184,33 @@ def tile_quaternionlinear_kernel(tc, x, Wr, Wi, Wj, Wk, br, bi, bj, bk, out):
                 for c in range(CHUNKS):
                     if HAMILTON[g][c] == (q, sign):
                         passes_done[c] += 1
-                        mx_pass(first_sums[c], 0, g, c, start=(passes_done[c] == 1), stop=(passes_done[c] == CHUNKS))
+                        mx_pass(
+                            first_sums[c], 0, g, c, 0, Q, start=(passes_done[c] == 1), stop=(passes_done[c] == CHUNKS)
+                        )
                         if passes_done[c] == CHUNKS:
                             closed.append(c)
             if LAST_REGROUP <= i <= LAST_REGROUP + 1:
-                x_values[i - LAST_REGROUP + 1] = transpose_x(i - LAST_REGROUP + 1)
+                a = i - LAST_REGROUP + 1
+                x_sorted[a + 2] = sort_x(a + 2)
+                x_values[a] = transpose_x(a, word_pairs(a))
         quantise_x(1, x_values[1])
         for c in closed:
-            finish(first_sums[c], 0, c)
+            finish(first_sums[c], 0, c, 0, Q)
 
+        LAST_PIECES = 2
         for m in range(1, ROW_TILES):
             if m % 2 == 1:
                 for a in range(m + 2, min(m + 4, ROW_TILES)):
-                    x_values[a] = transpose_x(a)
+                    x_values[a] = transpose_x(a, x_sorted[a])
+                for a in range(m + 4, min(m + 6, ROW_TILES)):
+                    x_sorted[a] = sort_x(a)
             if m + 1 < ROW_TILES:
                 quantise_x(m + 1, x_values[m + 1])
             for c in range(CHUNKS):
-                sums = sum_banks.tile([P, Q], F32, name="sums", tag="sums")
-                for g in range(CHUNKS):
-                    mx_pass(sums, m, g, c, start=(g == 0), stop=(g == CHUNKS - 1))
-                finish(sums, m, c)
+                pieces = LAST_PIECES if (m, c) == (ROW_TILES - 1, CHUNKS - 1) else 1
+                width = Q // pieces
+                for piece in range(pieces):
+                    sums = sum_banks.tile([P, width], F32, name="sums", tag="sums")
+                    for g in range(CHUNKS):
+                        mx_pass(sums, m, g, c, piece * width, width, start=(g == 0), stop=(g == CHUNKS - 1))
+                    finish(sums, m, c, piece * width, width)

@@ -23,7 +23,6 @@ HAMILTON = (
     ((2, -1), (3, -1), (0, 1), (1, 1)),
     ((3, -1), (2, 1), (1, -1), (0, 1)),
 )
-OPERANDS = ((0, 1), (1, 1), (2, 1), (3, 1), (1, -1), (2, -1), (3, -1))
 BIAS_SIGN = (
     (1, -1, -1, -1),
     (1, 1, 1, -1),
@@ -40,13 +39,15 @@ def tile_quaternionlinear_kernel(tc, x, Wr, Wi, Wj, Wk, br, bi, bj, bk, out):
     with ExitStack() as ctx:
         keep = ctx.enter_context(tc.tile_pool(name="keep", bufs=1))
         x_stage = ctx.enter_context(tc.tile_pool(name="x_stage", bufs=4))
-        w_stage = ctx.enter_context(tc.tile_pool(name="w_stage", bufs=2))
+        neg_stage = ctx.enter_context(tc.tile_pool(name="neg_stage", bufs=3))
         sort_stage = ctx.enter_context(tc.tile_pool(name="sort_stage", bufs=4))
-        out_stage = ctx.enter_context(tc.tile_pool(name="out_stage", bufs=6))
-        flip_banks = ctx.enter_context(tc.psum_pool(name="flip_banks", bufs=4))
-        sum_banks = ctx.enter_context(tc.psum_pool(name="sum_banks", bufs=4))
+        out_stage = ctx.enter_context(tc.tile_pool(name="out_stage", bufs=8))
+        psum = ctx.enter_context(tc.psum_pool(name="psum", bufs=1))
 
         ctx.enter_context(tc.manual_schedule())
+
+        def bank(b, shape):
+            return psum.tile(shape, F32, name="bank%d" % b, tag="bank%d" % b)
 
         identity = keep.tile([P, P], F32)
         bias_rows = keep.tile([P, Q], BF16)
@@ -55,10 +56,12 @@ def tile_quaternionlinear_kernel(tc, x, Wr, Wi, Wj, Wk, br, bi, bj, bk, out):
         x_rows = keep.tile([P, ROW_TILES, IN], BF16)
         x_codes = keep.tile([P, ROW_TILES, CHUNKS * P], U32, align_bytes=64)
         x_scales = keep.tile([P, ROW_TILES, CHUNKS * P], U8, align_bytes=64)
+        xn_codes = keep.tile([P, ROW_TILES, (CHUNKS - 1) * P], U32, align_bytes=64)
+        xn_scales = keep.tile([P, ROW_TILES, (CHUNKS - 1) * P], U8, align_bytes=64)
         w_rows = keep.tile([P, CHUNKS, PACK, Q], BF16)
         w_grouped = keep.tile([P, CHUNKS, Q, PACK], BF16, align_bytes=64)
-        w_codes = keep.tile([P, 2, CHUNKS, Q], U32, align_bytes=64)
-        w_scales = keep.tile([P, 2, CHUNKS, Q], U8, align_bytes=64)
+        w_codes = keep.tile([P, CHUNKS, Q], U32, align_bytes=64)
+        w_scales = keep.tile([P, CHUNKS, Q], U8, align_bytes=64)
 
         nc.gpsimd.memset(bias_rows[:].bitcast(F32), 0.0)
         make_identity(nc, identity[:])
@@ -80,53 +83,49 @@ def tile_quaternionlinear_kernel(tc, x, Wr, Wi, Wj, Wk, br, bi, bj, bk, out):
             nc.sync.dma_start(out=x_rows[:, m, :], in_=x[m * P : (m + 1) * P, :])
 
         load_x(0)
-        for q in range(CHUNKS):
+        load_weight(0)
+        load_x(1)
+        for q in range(1, CHUNKS):
             load_weight(q)
-        for m in range(1, ROW_TILES):
+        for m in range(2, ROW_TILES):
             load_x(m)
 
         def combine_bias():
             for c in range(CHUNKS):
-                bias_sum = sum_banks.tile([P, Q], F32, name="bias_sum", tag="sums")
+                bias_sum = bank(c, [P, Q])
                 nc.tensor.matmul(
                     out=bias_sum[:], lhsT=bias_signs[:, c, :], rhs=bias_rows[:], start=True, stop=True
                 )
                 copy = nc.vector.tensor_copy if c % 2 == 0 else nc.scalar.copy
                 copy(out=bias_all[:, c, :], in_=bias_sum[:])
 
-        def lay_out(q, sign):
-            plain = w_grouped[:, q, :, :].rearrange("p n t -> p (n t)")
-            if sign < 0:
-                negated = w_stage.tile([P, Q * PACK], BF16, align_bytes=64)
-                nc.vector.tensor_scalar_mul(out=negated[:], in0=plain, scalar1=-1.0)
-                return negated[:]
-            half = Q // 2
-            for copy, cols in ((nc.vector.tensor_copy, slice(0, half)), (nc.scalar.copy, slice(half, Q))):
+        def lay_out(q, vector_cols):
+            for copy, cols in ((nc.vector.tensor_copy, slice(0, vector_cols)), (nc.scalar.copy, slice(vector_cols, Q))):
                 copy(
                     out=w_grouped[:, q, cols, :].rearrange("p (c i) t -> p c t i", i=4),
                     in_=w_rows[:, q, :, cols].rearrange("p t (c i) -> p c t i", i=4),
                 )
-            return plain
 
-        def quantise_operand(q, sign, values):
-            s = 0 if sign > 0 else 1
+        def quantise_weight(q):
             nc.vector.quantize_mx(
-                out=w_codes[:, s, q, :].bitcast(FP8X4), scales=w_scales[:, s, q, :], in_=values
+                out=w_codes[:, q, :].bitcast(FP8X4),
+                scales=w_scales[:, q, :],
+                in_=w_grouped[:, q, :, :].rearrange("p n t -> p (n t)"),
             )
 
         def word_pairs(m):
             return x_rows[:, m, :].bitcast(F32).rearrange("p (g j u) -> p g u j", g=CHUNKS, u=2)
 
         def sort_x(m):
-            sorted_words = sort_stage.tile([P, CHUNKS, 2, P], F32)
+            sorted_words = sort_stage.tile([P, CHUNKS, 2, P], F32, name="sorted_words")
             nc.scalar.copy(out=sorted_words[:], in_=word_pairs(m))
             return sorted_words[:]
 
-        def transpose_x(m, words):
+        def transpose_x(words, banks):
             grouped = x_stage.tile([P, CHUNKS * P * PACK], BF16, align_bytes=64, name="x_grouped")
             grouped_words = grouped[:].bitcast(F32).rearrange("p (g r u) -> p g r u", g=CHUNKS, u=2)
             for h in range(2):
-                flipped = flip_banks.tile([P, 2, 2, P], F32, name="flipped", tag="flipped")
+                flipped = bank(banks[h], [P, 2, 2, P])
                 for gi in range(2):
                     for u in range(2):
                         nc.tensor.transpose(flipped[:, gi, u, :], words[:, 2 * h + gi, u, :], identity[:])
@@ -141,17 +140,35 @@ def tile_quaternionlinear_kernel(tc, x, Wr, Wi, Wj, Wk, br, bi, bj, bk, out):
                 out=x_codes[:, m, :].bitcast(FP8X4), scales=x_scales[:, m, :], in_=grouped[:]
             )
 
+        def negate_x(grouped):
+            negated = neg_stage.tile([P, (CHUNKS - 1) * P * PACK], BF16, align_bytes=64, name="x_negated")
+            nc.vector.tensor_scalar_mul(out=negated[:], in0=grouped[:, P * PACK :], scalar1=-1.0)
+            return negated
+
+        def quantise_negated(m, negated):
+            for words, values in (
+                (slice(0, 2 * P), slice(0, 2 * P * PACK)),
+                (slice(2 * P, 3 * P), slice(2 * P * PACK, 3 * P * PACK)),
+            ):
+                nc.vector.quantize_mx(
+                    out=xn_codes[:, m, words].bitcast(FP8X4), scales=xn_scales[:, m, words], in_=negated[:, values]
+                )
+
         def mx_pass(sums, m, g, c, first, width, start, stop):
             cols = slice(first, first + width)
             q, sign = HAMILTON[g][c]
-            s = 0 if sign > 0 else 1
-            rows = slice(g * P, (g + 1) * P)
+            if sign > 0:
+                rows = slice(g * P, (g + 1) * P)
+                codes, scales = x_codes, x_scales
+            else:
+                rows = slice((g - 1) * P, g * P)
+                codes, scales = xn_codes, xn_scales
             nc.tensor.matmul_mx(
                 out=sums[:],
-                lhsT=x_codes[:, m, rows].bitcast(FP8X4),
-                lhsT_scale=x_scales[:, m, rows],
-                rhs=w_codes[:, s, q, cols].bitcast(FP8X4),
-                rhs_scale=w_scales[:, s, q, cols],
+                lhsT=codes[:, m, rows].bitcast(FP8X4),
+                lhsT_scale=scales[:, m, rows],
+                rhs=w_codes[:, q, cols].bitcast(FP8X4),
+                rhs_scale=w_scales[:, q, cols],
                 start=start,
                 stop=stop,
             )
@@ -165,52 +182,107 @@ def tile_quaternionlinear_kernel(tc, x, Wr, Wi, Wj, Wk, br, bi, bj, bk, out):
                 out=out[m * P : (m + 1) * P, c * Q + first : c * Q + first + width], in_=result[:]
             )
 
-        combine_bias()
+        open_sums = {}
+        passes_done = {}
 
-        LAST_REGROUP = CHUNKS - 2
-        w_values = {0: lay_out(*OPERANDS[0])}
-        x_values = {0: transpose_x(0, word_pairs(0))}
-        x_sorted = {}
-        first_sums = [sum_banks.tile([P, Q], F32, name="sums", tag="sums") for c in range(CHUNKS)]
-        passes_done = [0] * CHUNKS
-        closed = []
-        for i, (q, sign) in enumerate(OPERANDS):
-            if i + 1 < len(OPERANDS):
-                w_values[i + 1] = lay_out(*OPERANDS[i + 1])
-            quantise_operand(q, sign, w_values[i])
-            if i == 0:
-                quantise_x(0, x_values[0])
-            for g in range(CHUNKS):
-                for c in range(CHUNKS):
+        def open_sum(m, c, b):
+            open_sums[(m, c)] = bank(b, [P, Q])
+            passes_done[(m, c)] = 0
+
+        def head_pass(m, g, c):
+            passes_done[(m, c)] += 1
+            mx_pass(
+                open_sums[(m, c)], m, g, c, 0, Q,
+                start=(passes_done[(m, c)] == 1), stop=(passes_done[(m, c)] == CHUNKS),
+            )
+
+        def head_passes(m, q, chunks):
+            for sign in (1, -1):
+                for c in chunks:
+                    for g in range(CHUNKS):
+                        if HAMILTON[g][c] == (q, sign):
+                            head_pass(m, g, c)
+
+        combine_bias()
+        xg = {}
+        xn = {}
+        xs = {}
+
+        def signed_passes(m, q, sign, chunks):
+            for c in chunks:
+                for g in range(CHUNKS):
                     if HAMILTON[g][c] == (q, sign):
-                        passes_done[c] += 1
-                        mx_pass(
-                            first_sums[c], 0, g, c, 0, Q, start=(passes_done[c] == 1), stop=(passes_done[c] == CHUNKS)
-                        )
-                        if passes_done[c] == CHUNKS:
-                            closed.append(c)
-            if LAST_REGROUP <= i <= LAST_REGROUP + 1:
-                a = i - LAST_REGROUP + 1
-                x_sorted[a + 2] = sort_x(a + 2)
-                x_values[a] = transpose_x(a, word_pairs(a))
-        quantise_x(1, x_values[1])
-        for c in closed:
-            finish(first_sums[c], 0, c, 0, Q)
+                        head_pass(m, g, c)
+
+        xg[0] = transpose_x(word_pairs(0), (4, 5))
+        lay_out(0, 384)
+        xg[1] = transpose_x(word_pairs(1), (6, 7))
+        quantise_x(0, xg[0])
+        quantise_weight(0)
+        for c in range(CHUNKS):
+            open_sum(0, c, c)
+        signed_passes(0, 0, 1, range(CHUNKS))
+        lay_out(1, 256)
+        quantise_x(1, xg[1])
+        open_sum(1, 2, 4)
+        open_sum(1, 3, 5)
+        signed_passes(1, 0, 1, (2, 3))
+        xn[0] = negate_x(xg[0])
+        quantise_weight(1)
+        signed_passes(0, 1, 1, range(CHUNKS))
+        signed_passes(1, 1, 1, (2, 3))
+        quantise_negated(0, xn[0])
+        signed_passes(0, 1, -1, range(CHUNKS))
+        lay_out(2, 256)
+        xn[1] = negate_x(xg[1])
+        quantise_weight(2)
+        lay_out(3, 128)
+        xg[2] = transpose_x(word_pairs(2), (6, 7))
+        signed_passes(0, 2, 1, range(CHUNKS))
+        signed_passes(1, 2, 1, (2, 3))
+        signed_passes(0, 2, -1, range(CHUNKS))
+        quantise_negated(1, xn[1])
+        signed_passes(1, 1, -1, (2, 3))
+        signed_passes(1, 2, -1, (2, 3))
+        xs[3] = sort_x(3)
+        xs[4] = sort_x(4)
+        quantise_weight(3)
+        for i, (m, c) in enumerate(((0, 0), (0, 1), (0, 2), (0, 3), (1, 2), (1, 3))):
+            head_passes(m, 3, (c,))
+            finish(open_sums[(m, c)], m, c, 0, Q)
+            if i == 1:
+                quantise_x(2, xg[2])
+                xn[2] = negate_x(xg[2])
+            if i == 3:
+                quantise_negated(2, xn[2])
+
+        def g_order(c):
+            return sorted(range(CHUNKS), key=lambda g: -HAMILTON[g][c][1])
+
+        def whole_chunk(m, c, b, first, width):
+            sums = bank(b, [P, width])
+            for i, g in enumerate(g_order(c)):
+                mx_pass(sums, m, g, c, first, width, start=(i == 0), stop=(i == CHUNKS - 1))
+            finish(sums, m, c, first, width)
+
+        whole_chunk(1, 0, 6, 0, Q)
+        whole_chunk(1, 1, 7, 0, Q)
 
         LAST_PIECES = 2
-        for m in range(1, ROW_TILES):
-            if m % 2 == 1:
-                for a in range(m + 2, min(m + 4, ROW_TILES)):
-                    x_values[a] = transpose_x(a, x_sorted[a])
-                for a in range(m + 4, min(m + 6, ROW_TILES)):
-                    x_sorted[a] = sort_x(a)
-            if m + 1 < ROW_TILES:
-                quantise_x(m + 1, x_values[m + 1])
+        for m in range(2, ROW_TILES):
+            if m % 2 == 0:
+                for i, a in enumerate(range(m + 1, min(m + 3, ROW_TILES))):
+                    xg[a] = transpose_x(xs[a], (2 * i, 2 * i + 1))
+                for a in range(m + 3, min(m + 5, ROW_TILES)):
+                    xs[a] = sort_x(a)
             for c in range(CHUNKS):
-                pieces = LAST_PIECES if (m, c) == (ROW_TILES - 1, CHUNKS - 1) else 1
-                width = Q // pieces
-                for piece in range(pieces):
-                    sums = sum_banks.tile([P, width], F32, name="sums", tag="sums")
-                    for g in range(CHUNKS):
-                        mx_pass(sums, m, g, c, piece * width, width, start=(g == 0), stop=(g == CHUNKS - 1))
-                    finish(sums, m, c, piece * width, width)
+                if (m, c) == (ROW_TILES - 1, CHUNKS - 1):
+                    whole_chunk(m, c, 7, 0, Q // 2)
+                    whole_chunk(m, c, 0, Q // 2, Q // 2)
+                else:
+                    whole_chunk(m, c, 4 + c, 0, Q)
+                if m + 1 < ROW_TILES and c == 0:
+                    quantise_x(m + 1, xg[m + 1])
+                    xn[m + 1] = negate_x(xg[m + 1])
+                if m + 1 < ROW_TILES and c == 1:
+                    quantise_negated(m + 1, xn[m + 1])

@@ -214,9 +214,18 @@ def tile_quaternionlinear_kernel(tc, x, Wr, Wi, Wj, Wk, br, bi, bj, bk, out):
                     if HAMILTON[g][c] == (q, sign):
                         head_pass(m, g, c)
 
+        def keep_warm(count, b):
+            for i in range(count):
+                unread = bank(b, [P, Q])
+                nc.tensor.matmul(
+                    out=unread[:], lhsT=bias_signs[:, 0, :], rhs=bias_rows[:], start=True, stop=True
+                )
+
         xg[0] = transpose_x(word_pairs(0), (4, 5))
+        keep_warm(2, 0)
         lay_out(0, 384)
         xg[1] = transpose_x(word_pairs(1), (6, 7))
+        keep_warm(2, 1)
         quantise_x(0, xg[0])
         quantise_weight(0)
         for c in range(CHUNKS):

@@ -15,6 +15,7 @@ B, IN, OUT = 1024, 2048, 2048
 Q = 512
 CHUNKS = 4
 ROW_TILES = B // P
+FIRST_TURNED = 7
 FLOPS = 2 * B * IN * OUT
 
 HAMILTON = (
@@ -38,10 +39,11 @@ def tile_quaternionlinear_kernel(tc, x, Wr, Wi, Wj, Wk, br, bi, bj, bk, out):
 
     with ExitStack() as ctx:
         keep = ctx.enter_context(tc.tile_pool(name="keep", bufs=1))
-        x_stage = ctx.enter_context(tc.tile_pool(name="x_stage", bufs=4))
+        x_stage = ctx.enter_context(tc.tile_pool(name="x_stage", bufs=5))
         neg_stage = ctx.enter_context(tc.tile_pool(name="neg_stage", bufs=3))
         sort_stage = ctx.enter_context(tc.tile_pool(name="sort_stage", bufs=4))
-        out_stage = ctx.enter_context(tc.tile_pool(name="out_stage", bufs=8))
+        turn_stage = ctx.enter_context(tc.tile_pool(name="turn_stage", bufs=1))
+        out_stage = ctx.enter_context(tc.tile_pool(name="out_stage", bufs=12))
         psum = ctx.enter_context(tc.psum_pool(name="psum", bufs=1))
 
         ctx.enter_context(tc.manual_schedule())
@@ -87,8 +89,22 @@ def tile_quaternionlinear_kernel(tc, x, Wr, Wi, Wj, Wk, br, bi, bj, bk, out):
         load_x(1)
         for q in range(1, CHUNKS):
             load_weight(q)
-        for m in range(2, ROW_TILES):
+        for m in range(2, FIRST_TURNED):
             load_x(m)
+
+        x_chunks = x.rearrange("b (g c) -> (b g) c", g=CHUNKS)
+
+        def load_x_quartered(m):
+            for a in range(4):
+                nc.sync.dma_start(
+                    out=x_rows[32 * a : 32 * a + 32, m, :].rearrange("s (e k) -> s e k", k=P),
+                    in_=x_chunks[m * P * CHUNKS : (m + 1) * P * CHUNKS, a * P : (a + 1) * P].rearrange(
+                        "(s e) k -> s e k", e=4 * CHUNKS
+                    ),
+                )
+
+        for m in range(FIRST_TURNED, ROW_TILES):
+            load_x_quartered(m)
 
         def combine_bias():
             for c in range(CHUNKS):
@@ -120,6 +136,31 @@ def tile_quaternionlinear_kernel(tc, x, Wr, Wi, Wj, Wk, br, bi, bj, bk, out):
             sorted_words = sort_stage.tile([P, CHUNKS, 2, P], F32, name="sorted_words")
             nc.scalar.copy(out=sorted_words[:], in_=word_pairs(m))
             return sorted_words[:]
+
+        def sort_quartered(m):
+            sorted_words = turn_stage.tile([P, 4 * CHUNKS, 2, 32], F32, align_bytes=64, name="sorted_quarters")
+            nc.scalar.copy(
+                out=sorted_words[:],
+                in_=x_rows[:, m, :].bitcast(F32).rearrange("p (e j u) -> p e u j", j=32, u=2),
+            )
+            return sorted_words
+
+        def turn_x(sorted_words):
+            turned = turn_stage.tile([P, 4, CHUNKS, 2, 32], F32, align_bytes=64, name="turned")
+            nc.vector.transpose(
+                out=turned[:].rearrange("p r g u s -> p (r g u s)"),
+                in_=sorted_words[:].rearrange("p e u j -> p (e u j)"),
+            )
+            return turned
+
+        def group_turned(turned):
+            grouped = x_stage.tile([P, CHUNKS * P * PACK], BF16, align_bytes=64, name="x_grouped")
+            grouped_words = grouped[:].bitcast(F32).rearrange("p (g s r u) -> p g s r u", g=CHUNKS, r=4, u=2)
+            for g in range(CHUNKS):
+                nc.scalar.copy(
+                    out=grouped_words[:, g, :, :, :], in_=turned[:, :, g, :, :].rearrange("p r u s -> p s r u")
+                )
+            return grouped
 
         def transpose_x(words, banks):
             grouped = x_stage.tile([P, CHUNKS * P * PACK], BF16, align_bytes=64, name="x_grouped")
@@ -280,9 +321,9 @@ def tile_quaternionlinear_kernel(tc, x, Wr, Wi, Wj, Wk, br, bi, bj, bk, out):
         LAST_PIECES = 2
         for m in range(2, ROW_TILES):
             if m % 2 == 0:
-                for i, a in enumerate(range(m + 1, min(m + 3, ROW_TILES))):
+                for i, a in enumerate(range(m + 1, min(m + 3, FIRST_TURNED))):
                     xg[a] = transpose_x(xs[a], (2 * i, 2 * i + 1))
-                for a in range(m + 3, min(m + 5, ROW_TILES)):
+                for a in range(m + 3, min(m + 5, FIRST_TURNED)):
                     xs[a] = sort_x(a)
             for c in range(CHUNKS):
                 if (m, c) == (ROW_TILES - 1, CHUNKS - 1):
@@ -295,3 +336,7 @@ def tile_quaternionlinear_kernel(tc, x, Wr, Wi, Wj, Wk, br, bi, bj, bk, out):
                     xn[m + 1] = negate_x(xg[m + 1])
                 if m + 1 < ROW_TILES and c == 1:
                     quantise_negated(m + 1, xn[m + 1])
+                if c == 3 and FIRST_TURNED <= m + 5 < ROW_TILES:
+                    xs[m + 5] = sort_quartered(m + 5)
+                if c == 0 and FIRST_TURNED <= m + 4 < ROW_TILES:
+                    xg[m + 4] = group_turned(turn_x(xs[m + 4]))

@@ -15,7 +15,7 @@ B, IN, OUT = 1024, 2048, 2048
 Q = 512
 CHUNKS = 4
 ROW_TILES = B // P
-FIRST_TURNED = 7
+FIRST_TURNED = 6
 FLOPS = 2 * B * IN * OUT
 
 HAMILTON = (
@@ -42,7 +42,7 @@ def tile_quaternionlinear_kernel(tc, x, Wr, Wi, Wj, Wk, br, bi, bj, bk, out):
         x_stage = ctx.enter_context(tc.tile_pool(name="x_stage", bufs=5))
         neg_stage = ctx.enter_context(tc.tile_pool(name="neg_stage", bufs=3))
         sort_stage = ctx.enter_context(tc.tile_pool(name="sort_stage", bufs=4))
-        turn_stage = ctx.enter_context(tc.tile_pool(name="turn_stage", bufs=1))
+        turn_stage = ctx.enter_context(tc.tile_pool(name="turn_stage", bufs=2))
         out_stage = ctx.enter_context(tc.tile_pool(name="out_stage", bufs=12))
         psum = ctx.enter_context(tc.psum_pool(name="psum", bufs=1))
 
@@ -318,6 +318,8 @@ def tile_quaternionlinear_kernel(tc, x, Wr, Wi, Wj, Wk, br, bi, bj, bk, out):
         whole_chunk(1, 0, 6, 0, Q)
         whole_chunk(1, 1, 7, 0, Q)
 
+        SORT_AT = {6: (2, 1), 7: (4, 0)}
+        TURN_AT = {6: (2, 3), 7: (4, 2)}
         LAST_PIECES = 2
         for m in range(2, ROW_TILES):
             if m % 2 == 0:
@@ -325,18 +327,23 @@ def tile_quaternionlinear_kernel(tc, x, Wr, Wi, Wj, Wk, br, bi, bj, bk, out):
                     xg[a] = transpose_x(xs[a], (2 * i, 2 * i + 1))
                 for a in range(m + 3, min(m + 5, FIRST_TURNED)):
                     xs[a] = sort_x(a)
+            ahead = m + 1 < ROW_TILES and (m % 2 == 1 or m + 1 >= FIRST_TURNED)
+            if ahead:
+                quantise_x(m + 1, xg[m + 1])
+                xn[m + 1] = negate_x(xg[m + 1])
             for c in range(CHUNKS):
                 if (m, c) == (ROW_TILES - 1, CHUNKS - 1):
                     whole_chunk(m, c, 7, 0, Q // 2)
                     whole_chunk(m, c, 0, Q // 2, Q // 2)
                 else:
-                    whole_chunk(m, c, 4 + c, 0, Q)
-                if m + 1 < ROW_TILES and c == 0:
+                    whole_chunk(m, c, c if m == ROW_TILES - 2 else 4 + c, 0, Q)
+                if m + 1 < ROW_TILES and c == 0 and not ahead:
                     quantise_x(m + 1, xg[m + 1])
                     xn[m + 1] = negate_x(xg[m + 1])
-                if m + 1 < ROW_TILES and c == 1:
+                if m + 1 < ROW_TILES and c == (0 if ahead else 1):
                     quantise_negated(m + 1, xn[m + 1])
-                if c == 3 and FIRST_TURNED <= m + 5 < ROW_TILES:
-                    xs[m + 5] = sort_quartered(m + 5)
-                if c == 0 and FIRST_TURNED <= m + 4 < ROW_TILES:
-                    xg[m + 4] = group_turned(turn_x(xs[m + 4]))
+                for a in range(FIRST_TURNED, ROW_TILES):
+                    if SORT_AT[a] == (m, c):
+                        xs[a] = sort_quartered(a)
+                    if TURN_AT[a] == (m, c):
+                        xg[a] = group_turned(turn_x(xs[a]))

@@ -15,7 +15,7 @@ B, IN, OUT = 1024, 2048, 2048
 Q = 512
 CHUNKS = 4
 ROW_TILES = B // P
-FIRST_TURNED = 6
+FIRST_TURNED = 5
 FLOPS = 2 * B * IN * OUT
 
 HAMILTON = (
@@ -40,9 +40,9 @@ def tile_quaternionlinear_kernel(tc, x, Wr, Wi, Wj, Wk, br, bi, bj, bk, out):
     with ExitStack() as ctx:
         keep = ctx.enter_context(tc.tile_pool(name="keep", bufs=1))
         x_stage = ctx.enter_context(tc.tile_pool(name="x_stage", bufs=5))
-        neg_stage = ctx.enter_context(tc.tile_pool(name="neg_stage", bufs=3))
+        neg_stage = ctx.enter_context(tc.tile_pool(name="neg_stage", bufs=5))
         sort_stage = ctx.enter_context(tc.tile_pool(name="sort_stage", bufs=4))
-        turn_stage = ctx.enter_context(tc.tile_pool(name="turn_stage", bufs=2))
+        turn_stage = ctx.enter_context(tc.tile_pool(name="turn_stage", bufs=3))
         out_stage = ctx.enter_context(tc.tile_pool(name="out_stage", bufs=12))
         psum = ctx.enter_context(tc.psum_pool(name="psum", bufs=1))
 
@@ -181,9 +181,12 @@ def tile_quaternionlinear_kernel(tc, x, Wr, Wi, Wj, Wk, br, bi, bj, bk, out):
                 out=x_codes[:, m, :].bitcast(FP8X4), scales=x_scales[:, m, :], in_=grouped[:]
             )
 
-        def negate_x(grouped):
+        def negate_x(grouped, on_scalar=False):
             negated = neg_stage.tile([P, (CHUNKS - 1) * P * PACK], BF16, align_bytes=64, name="x_negated")
-            nc.vector.tensor_scalar_mul(out=negated[:], in0=grouped[:, P * PACK :], scalar1=-1.0)
+            if on_scalar:
+                nc.scalar.mul(out=negated[:], in_=grouped[:, P * PACK :], mul=-1.0)
+            else:
+                nc.vector.tensor_scalar_mul(out=negated[:], in0=grouped[:, P * PACK :], scalar1=-1.0)
             return negated
 
         def quantise_negated(m, negated):
@@ -318,8 +321,8 @@ def tile_quaternionlinear_kernel(tc, x, Wr, Wi, Wj, Wk, br, bi, bj, bk, out):
         whole_chunk(1, 0, 6, 0, Q)
         whole_chunk(1, 1, 7, 0, Q)
 
-        SORT_AT = {6: (2, 1), 7: (4, 0)}
-        TURN_AT = {6: (2, 3), 7: (4, 2)}
+        SORT_AT = {5: (2, 0), 6: (2, 0), 7: (2, 2)}
+        TURN_AT = {5: (2, 1), 6: (3, 1), 7: (4, 1)}
         LAST_PIECES = 2
         for m in range(2, ROW_TILES):
             if m % 2 == 0:
@@ -330,13 +333,14 @@ def tile_quaternionlinear_kernel(tc, x, Wr, Wi, Wj, Wk, br, bi, bj, bk, out):
             ahead = m + 1 < ROW_TILES and (m % 2 == 1 or m + 1 >= FIRST_TURNED)
             if ahead:
                 quantise_x(m + 1, xg[m + 1])
-                xn[m + 1] = negate_x(xg[m + 1])
+                if m + 1 < FIRST_TURNED:
+                    xn[m + 1] = negate_x(xg[m + 1])
             for c in range(CHUNKS):
                 if (m, c) == (ROW_TILES - 1, CHUNKS - 1):
-                    whole_chunk(m, c, 7, 0, Q // 2)
-                    whole_chunk(m, c, 0, Q // 2, Q // 2)
+                    whole_chunk(m, c, 3, 0, Q // 2)
+                    whole_chunk(m, c, 4, Q // 2, Q // 2)
                 else:
-                    whole_chunk(m, c, c if m == ROW_TILES - 2 else 4 + c, 0, Q)
+                    whole_chunk(m, c, c if m % 2 == 1 else 4 + c, 0, Q)
                 if m + 1 < ROW_TILES and c == 0 and not ahead:
                     quantise_x(m + 1, xg[m + 1])
                     xn[m + 1] = negate_x(xg[m + 1])
@@ -347,3 +351,4 @@ def tile_quaternionlinear_kernel(tc, x, Wr, Wi, Wj, Wk, br, bi, bj, bk, out):
                         xs[a] = sort_quartered(a)
                     if TURN_AT[a] == (m, c):
                         xg[a] = group_turned(turn_x(xs[a]))
+                        xn[a] = negate_x(xg[a], on_scalar=True)

@@ -40,7 +40,7 @@ def tile_quaternionlinear_kernel(tc, x, Wr, Wi, Wj, Wk, br, bi, bj, bk, out):
     with ExitStack() as ctx:
         keep = ctx.enter_context(tc.tile_pool(name="keep", bufs=1))
         x_stage = ctx.enter_context(tc.tile_pool(name="x_stage", bufs=5))
-        neg_stage = ctx.enter_context(tc.tile_pool(name="neg_stage", bufs=5))
+        neg_stage = ctx.enter_context(tc.tile_pool(name="neg_stage", bufs=3))
         sort_stage = ctx.enter_context(tc.tile_pool(name="sort_stage", bufs=4))
         turn_stage = ctx.enter_context(tc.tile_pool(name="turn_stage", bufs=3))
         out_stage = ctx.enter_context(tc.tile_pool(name="out_stage", bufs=12))
@@ -181,12 +181,9 @@ def tile_quaternionlinear_kernel(tc, x, Wr, Wi, Wj, Wk, br, bi, bj, bk, out):
                 out=x_codes[:, m, :].bitcast(FP8X4), scales=x_scales[:, m, :], in_=grouped[:]
             )
 
-        def negate_x(grouped, on_scalar=False):
+        def negate_x(grouped):
             negated = neg_stage.tile([P, (CHUNKS - 1) * P * PACK], BF16, align_bytes=64, name="x_negated")
-            if on_scalar:
-                nc.scalar.mul(out=negated[:], in_=grouped[:, P * PACK :], mul=-1.0)
-            else:
-                nc.vector.tensor_scalar_mul(out=negated[:], in0=grouped[:, P * PACK :], scalar1=-1.0)
+            nc.vector.tensor_scalar_mul(out=negated[:], in0=grouped[:, P * PACK :], scalar1=-1.0)
             return negated
 
         def quantise_negated(m, negated):
@@ -333,8 +330,7 @@ def tile_quaternionlinear_kernel(tc, x, Wr, Wi, Wj, Wk, br, bi, bj, bk, out):
             ahead = m + 1 < ROW_TILES and (m % 2 == 1 or m + 1 >= FIRST_TURNED)
             if ahead:
                 quantise_x(m + 1, xg[m + 1])
-                if m + 1 < FIRST_TURNED:
-                    xn[m + 1] = negate_x(xg[m + 1])
+                xn[m + 1] = negate_x(xg[m + 1])
             for c in range(CHUNKS):
                 if (m, c) == (ROW_TILES - 1, CHUNKS - 1):
                     whole_chunk(m, c, 3, 0, Q // 2)
@@ -351,4 +347,3 @@ def tile_quaternionlinear_kernel(tc, x, Wr, Wi, Wj, Wk, br, bi, bj, bk, out):
                         xs[a] = sort_quartered(a)
                     if TURN_AT[a] == (m, c):
                         xg[a] = group_turned(turn_x(xs[a]))
-                        xn[a] = negate_x(xg[a], on_scalar=True)

@@ -56,14 +56,14 @@ def tile_quaternionlinear_kernel(tc, x, Wr, Wi, Wj, Wk, br, bi, bj, bk, out):
         bias_signs = keep.tile([P, CHUNKS, P], BF16)
         bias_all = keep.tile([P, CHUNKS, Q], F32)
         x_rows = keep.tile([P, ROW_TILES, IN], BF16)
-        x_codes = keep.tile([P, ROW_TILES, CHUNKS * P], U32, align_bytes=64)
-        x_scales = keep.tile([P, ROW_TILES, CHUNKS * P], U8, align_bytes=64)
-        xn_codes = keep.tile([P, ROW_TILES, (CHUNKS - 1) * P], U32, align_bytes=64)
-        xn_scales = keep.tile([P, ROW_TILES, (CHUNKS - 1) * P], U8, align_bytes=64)
+        x_codes = keep.tile([P, ROW_TILES, CHUNKS * P], U32, align_bytes=256)
+        x_scales = keep.tile([P, ROW_TILES, CHUNKS * P], U8, align_bytes=256)
+        xn_codes = keep.tile([P, ROW_TILES, (CHUNKS - 1) * P], U32, align_bytes=256)
+        xn_scales = keep.tile([P, ROW_TILES, (CHUNKS - 1) * P], U8, align_bytes=256)
         w_rows = keep.tile([P, CHUNKS, PACK, Q], BF16)
         w_grouped = keep.tile([P, CHUNKS, Q, PACK], BF16, align_bytes=64)
-        w_codes = keep.tile([P, CHUNKS, Q], U32, align_bytes=64)
-        w_scales = keep.tile([P, CHUNKS, Q], U8, align_bytes=64)
+        w_codes = keep.tile([P, CHUNKS, Q], U32, align_bytes=256)
+        w_scales = keep.tile([P, CHUNKS, Q], U8, align_bytes=256)
 
         nc.gpsimd.memset(bias_rows[:].bitcast(F32), 0.0)
         make_identity(nc, identity[:])

@@ -16,6 +16,7 @@ Q = 512
 CHUNKS = 4
 ROW_TILES = B // P
 FIRST_TURNED = 5
+NEGATED_TILES = 3
 FLOPS = 2 * B * IN * OUT
 
 HAMILTON = (
@@ -41,7 +42,7 @@ def tile_quaternionlinear_kernel(tc, x, Wr, Wi, Wj, Wk, br, bi, bj, bk, out):
         keep = ctx.enter_context(tc.tile_pool(name="keep", bufs=1))
         x_stage = ctx.enter_context(tc.tile_pool(name="x_stage", bufs=5))
         neg_stage = ctx.enter_context(tc.tile_pool(name="neg_stage", bufs=3))
-        sort_stage = ctx.enter_context(tc.tile_pool(name="sort_stage", bufs=4))
+        sort_stage = ctx.enter_context(tc.tile_pool(name="sort_stage", bufs=2))
         turn_stage = ctx.enter_context(tc.tile_pool(name="turn_stage", bufs=3))
         out_stage = ctx.enter_context(tc.tile_pool(name="out_stage", bufs=12))
         psum = ctx.enter_context(tc.psum_pool(name="psum", bufs=1))
@@ -53,28 +54,25 @@ def tile_quaternionlinear_kernel(tc, x, Wr, Wi, Wj, Wk, br, bi, bj, bk, out):
 
         identity = keep.tile([P, P], F32)
         bias_rows = keep.tile([P, Q], BF16)
+        idle_values = keep.tile([P, Q], BF16)
         bias_signs = keep.tile([P, CHUNKS, P], BF16)
         bias_all = keep.tile([P, CHUNKS, Q], F32)
         x_rows = keep.tile([P, ROW_TILES, IN], BF16)
         x_codes = keep.tile([P, ROW_TILES, CHUNKS * P], U32, align_bytes=256)
         x_scales = keep.tile([P, ROW_TILES, CHUNKS * P], U8, align_bytes=256)
-        xn_codes = keep.tile([P, ROW_TILES, (CHUNKS - 1) * P], U32, align_bytes=256)
-        xn_scales = keep.tile([P, ROW_TILES, (CHUNKS - 1) * P], U8, align_bytes=256)
+        xn_codes = keep.tile([P, NEGATED_TILES, (CHUNKS - 1) * P], U32, align_bytes=256)
+        xn_scales = keep.tile([P, NEGATED_TILES, (CHUNKS - 1) * P], U8, align_bytes=256)
         w_rows = keep.tile([P, CHUNKS, PACK, Q], BF16)
         w_grouped = keep.tile([P, CHUNKS, Q, PACK], BF16, align_bytes=64)
         w_codes = keep.tile([P, CHUNKS, Q], U32, align_bytes=256)
         w_scales = keep.tile([P, CHUNKS, Q], U8, align_bytes=256)
+        wn_codes = keep.tile([P, CHUNKS - 1, Q], U32, align_bytes=256)
+        wn_scales = keep.tile([P, CHUNKS - 1, Q], U8, align_bytes=256)
 
         nc.gpsimd.memset(bias_rows[:].bitcast(F32), 0.0)
-        make_identity(nc, identity[:])
         for c in range(CHUNKS):
             for v in range(4):
                 nc.vector.memset(bias_signs[32 * v : 32 * v + 32, c, :], float(BIAS_SIGN[c][v]))
-
-        for v in range(4):
-            nc.sync.dma_start(
-                out=bias_rows[32 * v : 32 * v + 1, :], in_=biases[v].rearrange("(o n) -> o n", o=1)
-            )
 
         def load_weight(q):
             nc.sync.dma_start(
@@ -84,13 +82,9 @@ def tile_quaternionlinear_kernel(tc, x, Wr, Wi, Wj, Wk, br, bi, bj, bk, out):
         def load_x(m):
             nc.sync.dma_start(out=x_rows[:, m, :], in_=x[m * P : (m + 1) * P, :])
 
-        load_x(0)
-        load_weight(0)
-        load_x(1)
-        for q in range(1, CHUNKS):
-            load_weight(q)
-        for m in range(2, FIRST_TURNED):
-            load_x(m)
+        def load_x_half(m, h):
+            cols = slice(h * IN // 2, (h + 1) * IN // 2)
+            nc.sync.dma_start(out=x_rows[:, m, cols], in_=x[m * P : (m + 1) * P, cols])
 
         x_chunks = x.rearrange("b (g c) -> (b g) c", g=CHUNKS)
 
@@ -103,30 +97,60 @@ def tile_quaternionlinear_kernel(tc, x, Wr, Wi, Wj, Wk, br, bi, bj, bk, out):
                     ),
                 )
 
+        for v in range(4):
+            nc.sync.dma_start(
+                out=bias_rows[32 * v : 32 * v + 1, :], in_=biases[v].rearrange("(o n) -> o n", o=1)
+            )
+        load_x_half(0, 0)
+        load_weight(0)
+        load_x_half(0, 1)
+        load_x(1)
+        load_weight(1)
+        load_x(2)
+        load_weight(2)
+        load_weight(3)
+        for m in range(3, FIRST_TURNED):
+            load_x(m)
         for m in range(FIRST_TURNED, ROW_TILES):
             load_x_quartered(m)
 
-        def combine_bias():
-            for c in range(CHUNKS):
-                bias_sum = bank(c, [P, Q])
-                nc.tensor.matmul(
-                    out=bias_sum[:], lhsT=bias_signs[:, c, :], rhs=bias_rows[:], start=True, stop=True
-                )
-                copy = nc.vector.tensor_copy if c % 2 == 0 else nc.scalar.copy
-                copy(out=bias_all[:, c, :], in_=bias_sum[:])
+        nc.gpsimd.memset(idle_values[:].bitcast(F32), 0.0)
+        make_identity(nc, identity[:])
 
-        def lay_out(q, vector_cols):
-            for copy, cols in ((nc.vector.tensor_copy, slice(0, vector_cols)), (nc.scalar.copy, slice(vector_cols, Q))):
-                copy(
-                    out=w_grouped[:, q, cols, :].rearrange("p (c i) t -> p c t i", i=4),
-                    in_=w_rows[:, q, :, cols].rearrange("p t (c i) -> p c t i", i=4),
-                )
+        def bias_sum(c):
+            sums = bank(c, [P, Q])
+            nc.tensor.matmul(
+                out=sums[:], lhsT=bias_signs[:, c, :], rhs=bias_rows[:], start=True, stop=True
+            )
+            return sums
+
+        def lay_out(q, copy, cols):
+            copy(
+                out=w_grouped[:, q, cols, :].rearrange("p (c i) t -> p c t i", i=4),
+                in_=w_rows[:, q, :, cols].rearrange("p t (c i) -> p c t i", i=4),
+            )
+
+        def lay_out_vector(q, n):
+            lay_out(q, nc.vector.tensor_copy, slice(0, n))
+
+        def lay_out_scalar(q, n):
+            lay_out(q, nc.scalar.copy, slice(n, Q))
 
         def quantise_weight(q):
             nc.vector.quantize_mx(
                 out=w_codes[:, q, :].bitcast(FP8X4),
                 scales=w_scales[:, q, :],
                 in_=w_grouped[:, q, :, :].rearrange("p n t -> p (n t)"),
+            )
+
+        def negate_weight(q):
+            negated = neg_stage.tile([P, Q * PACK], BF16, align_bytes=64, name="w_negated")
+            nc.scalar.mul(negated[:], w_grouped[:, q, :, :].rearrange("p n t -> p (n t)"), -1.0)
+            return negated
+
+        def quantise_negated_weight(q, negated):
+            nc.vector.quantize_mx(
+                out=wn_codes[:, q - 1, :].bitcast(FP8X4), scales=wn_scales[:, q - 1, :], in_=negated[:]
             )
 
         def word_pairs(m):
@@ -162,19 +186,33 @@ def tile_quaternionlinear_kernel(tc, x, Wr, Wi, Wj, Wk, br, bi, bj, bk, out):
                 )
             return grouped
 
-        def transpose_x(words, banks):
-            grouped = x_stage.tile([P, CHUNKS * P * PACK], BF16, align_bytes=64, name="x_grouped")
+        def new_group():
+            return x_stage.tile([P, CHUNKS * P * PACK], BF16, align_bytes=64, name="x_grouped")
+
+        def transpose_half(words, grouped, h, b):
             grouped_words = grouped[:].bitcast(F32).rearrange("p (g r u) -> p g r u", g=CHUNKS, u=2)
+            flipped = bank(b, [P, 2, 2, P])
+            for gi in range(2):
+                for u in range(2):
+                    nc.tensor.transpose(flipped[:, gi, u, :], words[:, 2 * h + gi, u, :], identity[:])
+            nc.scalar.copy(
+                out=grouped_words[:, 2 * h : 2 * h + 2, :, :],
+                in_=flipped[:].rearrange("p g u r -> p g r u"),
+            )
+
+        def transpose_x(words, banks):
+            grouped = new_group()
             for h in range(2):
-                flipped = bank(banks[h], [P, 2, 2, P])
-                for gi in range(2):
-                    for u in range(2):
-                        nc.tensor.transpose(flipped[:, gi, u, :], words[:, 2 * h + gi, u, :], identity[:])
-                nc.scalar.copy(
-                    out=grouped_words[:, 2 * h : 2 * h + 2, :, :],
-                    in_=flipped[:].rearrange("p g u r -> p g r u"),
-                )
+                transpose_half(words, grouped, h, banks[h])
             return grouped
+
+        def quantise_half(m, grouped, h):
+            words = slice(2 * h * P, 2 * (h + 1) * P)
+            nc.vector.quantize_mx(
+                out=x_codes[:, m, words].bitcast(FP8X4),
+                scales=x_scales[:, m, words],
+                in_=grouped[:, 2 * h * P * PACK : 2 * (h + 1) * P * PACK],
+            )
 
         def quantise_x(m, grouped):
             nc.vector.quantize_mx(
@@ -198,18 +236,19 @@ def tile_quaternionlinear_kernel(tc, x, Wr, Wi, Wj, Wk, br, bi, bj, bk, out):
         def mx_pass(sums, m, g, c, first, width, start, stop):
             cols = slice(first, first + width)
             q, sign = HAMILTON[g][c]
-            if sign > 0:
-                rows = slice(g * P, (g + 1) * P)
-                codes, scales = x_codes, x_scales
-            else:
+            stationary = (x_codes[:, m, g * P : (g + 1) * P], x_scales[:, m, g * P : (g + 1) * P])
+            moving = (w_codes[:, q, cols], w_scales[:, q, cols])
+            if sign < 0 and m < NEGATED_TILES:
                 rows = slice((g - 1) * P, g * P)
-                codes, scales = xn_codes, xn_scales
+                stationary = (xn_codes[:, m, rows], xn_scales[:, m, rows])
+            elif sign < 0:
+                moving = (wn_codes[:, q - 1, cols], wn_scales[:, q - 1, cols])
             nc.tensor.matmul_mx(
                 out=sums[:],
-                lhsT=codes[:, m, rows].bitcast(FP8X4),
-                lhsT_scale=scales[:, m, rows],
-                rhs=w_codes[:, q, cols].bitcast(FP8X4),
-                rhs_scale=w_scales[:, q, cols],
+                lhsT=stationary[0].bitcast(FP8X4),
+                lhsT_scale=stationary[1],
+                rhs=moving[0].bitcast(FP8X4),
+                rhs_scale=moving[1],
                 start=start,
                 stop=stop,
             )
@@ -230,81 +269,107 @@ def tile_quaternionlinear_kernel(tc, x, Wr, Wi, Wj, Wk, br, bi, bj, bk, out):
             open_sums[(m, c)] = bank(b, [P, Q])
             passes_done[(m, c)] = 0
 
-        def head_pass(m, g, c):
-            passes_done[(m, c)] += 1
-            mx_pass(
-                open_sums[(m, c)], m, g, c, 0, Q,
-                start=(passes_done[(m, c)] == 1), stop=(passes_done[(m, c)] == CHUNKS),
-            )
-
-        def head_passes(m, q, chunks):
-            for sign in (1, -1):
-                for c in chunks:
-                    for g in range(CHUNKS):
-                        if HAMILTON[g][c] == (q, sign):
-                            head_pass(m, g, c)
-
-        combine_bias()
-        xg = {}
-        xn = {}
-        xs = {}
-
         def signed_passes(m, q, sign, chunks):
             for c in chunks:
                 for g in range(CHUNKS):
                     if HAMILTON[g][c] == (q, sign):
-                        head_pass(m, g, c)
+                        passes_done[(m, c)] += 1
+                        mx_pass(
+                            open_sums[(m, c)], m, g, c, 0, Q,
+                            start=(passes_done[(m, c)] == 1), stop=(passes_done[(m, c)] == CHUNKS),
+                        )
+
+        ALL = range(CHUNKS)
+        xg = {}
+        xn = {}
+        xs = {}
+        wn = {}
 
         def keep_warm(count, b):
             for i in range(count):
                 unread = bank(b, [P, Q])
                 nc.tensor.matmul(
-                    out=unread[:], lhsT=bias_signs[:, 0, :], rhs=bias_rows[:], start=True, stop=True
+                    out=unread[:], lhsT=idle_values[:, 0:P], rhs=idle_values[:], start=True, stop=True
                 )
 
-        xg[0] = transpose_x(word_pairs(0), (4, 5))
+        def negw_vector(q):
+            negated = neg_stage.tile([P, Q * PACK], BF16, align_bytes=64, name="w_negated")
+            nc.vector.tensor_scalar_mul(
+                out=negated[:], in0=w_grouped[:, q, :, :].rearrange("p n t -> p (n t)"), scalar1=-1.0
+            )
+            wn[q] = negated
+
+        to_drain = []
+
+        def drain():
+            finish(*to_drain.pop(0))
+
+        keep_warm(3, 7)
+        sums = [bias_sum(c) for c in range(CHUNKS)]
+        for c in range(CHUNKS):
+            copy = nc.scalar.copy if c == 0 else nc.vector.tensor_copy
+            copy(out=bias_all[:, c, :], in_=sums[c][:])
+        xg[0] = new_group()
+        transpose_half(word_pairs(0), xg[0], 0, 4)
+        lay_out_scalar(0, 256)
+        lay_out_vector(0, 256)
+        transpose_half(word_pairs(0), xg[0], 1, 5)
         keep_warm(2, 0)
-        lay_out(0, 384)
+        quantise_half(0, xg[0], 0)
+        quantise_weight(0)
+        quantise_half(0, xg[0], 1)
         xg[1] = transpose_x(word_pairs(1), (6, 7))
         keep_warm(2, 1)
-        quantise_x(0, xg[0])
-        quantise_weight(0)
-        for c in range(CHUNKS):
-            open_sum(0, c, c)
-        signed_passes(0, 0, 1, range(CHUNKS))
-        lay_out(1, 256)
+        lay_out_scalar(1, 256)
+        lay_out_vector(1, 256)
         quantise_x(1, xg[1])
-        open_sum(1, 2, 4)
-        open_sum(1, 3, 5)
-        signed_passes(1, 0, 1, (2, 3))
         xn[0] = negate_x(xg[0])
         quantise_weight(1)
-        signed_passes(0, 1, 1, range(CHUNKS))
-        signed_passes(1, 1, 1, (2, 3))
+        for c in ALL:
+            open_sum(0, c, c)
+        signed_passes(0, 0, 1, ALL)
+        xg[2] = transpose_x(word_pairs(2), (4, 5))
+        lay_out_scalar(2, 256)
         quantise_negated(0, xn[0])
-        signed_passes(0, 1, -1, range(CHUNKS))
-        lay_out(2, 256)
+        open_sum(1, 2, 6)
+        open_sum(1, 3, 7)
+        signed_passes(1, 0, 1, (2, 3))
+        signed_passes(0, 1, 1, ALL)
+        signed_passes(1, 1, 1, (2, 3))
+        signed_passes(0, 1, -1, ALL)
+        open_sum(1, 0, 4)
+        open_sum(1, 1, 5)
+        signed_passes(1, 0, 1, (0, 1))
+        signed_passes(1, 1, 1, (0, 1))
+        lay_out_vector(2, 256)
         xn[1] = negate_x(xg[1])
         quantise_weight(2)
-        lay_out(3, 128)
-        xg[2] = transpose_x(word_pairs(2), (6, 7))
-        signed_passes(0, 2, 1, range(CHUNKS))
-        signed_passes(1, 2, 1, (2, 3))
-        signed_passes(0, 2, -1, range(CHUNKS))
+        signed_passes(0, 2, 1, ALL)
+        signed_passes(0, 2, -1, ALL)
+        signed_passes(1, 2, 1, ALL)
         quantise_negated(1, xn[1])
-        signed_passes(1, 1, -1, (2, 3))
-        signed_passes(1, 2, -1, (2, 3))
-        xs[3] = sort_x(3)
-        xs[4] = sort_x(4)
+        signed_passes(1, 1, -1, ALL)
+        signed_passes(1, 2, -1, ALL)
+        lay_out_vector(3, 128)
+        lay_out_scalar(3, 128)
+        xn[2] = negate_x(xg[2])
         quantise_weight(3)
-        for i, (m, c) in enumerate(((0, 0), (0, 1), (0, 2), (0, 3), (1, 2), (1, 3))):
-            head_passes(m, 3, (c,))
-            finish(open_sums[(m, c)], m, c, 0, Q)
-            if i == 1:
-                quantise_x(2, xg[2])
-                xn[2] = negate_x(xg[2])
-            if i == 3:
-                quantise_negated(2, xn[2])
+        quantise_x(2, xg[2])
+        xs[3] = sort_x(3)
+        negw_vector(3)
+        negw_vector(1)
+        xs[4] = sort_x(4)
+        wn[2] = negate_weight(2)
+        for m in range(2):
+            for c in ALL:
+                signed_passes(m, 3, 1, (c,))
+                signed_passes(m, 3, -1, (c,))
+                to_drain.append((open_sums[(m, c)], m, c, 0, Q))
+                if (m, c) == (0, 0):
+                    drain()
+                    quantise_negated(2, xn[2])
+                elif m == 0:
+                    drain()
 
         def g_order(c):
             return sorted(range(CHUNKS), key=lambda g: -HAMILTON[g][c][1])
@@ -315,35 +380,45 @@ def tile_quaternionlinear_kernel(tc, x, Wr, Wi, Wj, Wk, br, bi, bj, bk, out):
                 mx_pass(sums, m, g, c, first, width, start=(i == 0), stop=(i == CHUNKS - 1))
             finish(sums, m, c, first, width)
 
-        whole_chunk(1, 0, 6, 0, Q)
-        whole_chunk(1, 1, 7, 0, Q)
+        taken = [0]
 
-        SORT_AT = {5: (2, 0), 6: (2, 0), 7: (2, 2)}
-        TURN_AT = {5: (2, 1), 6: (3, 1), 7: (4, 1)}
-        LAST_PIECES = 2
+        def next_bank():
+            taken[0] += 1
+            return (taken[0] - 1) % 8
+
+        def step(s):
+            k, a = s[0], int(s[1:] or 0)
+            if k == "d":
+                drain()
+            if k == "q":
+                quantise_x(a, xg[a])
+            if k == "n":
+                quantise_negated_weight(a, wn[a])
+            if k == "t":
+                xs[a] = turn_x(xs[a])
+            if k == "c":
+                xg[a] = group_turned(xs[a])
+            if k == "s":
+                xs[a] = sort_quartered(a) if a >= FIRST_TURNED else sort_x(a)
+            if k == "f":
+                xg[a] = transpose_x(xs[a], (next_bank(), next_bank()))
+            if k == "w":
+                wn[a] = negate_weight(a)
+            if k == "v":
+                negw_vector(a)
+        STEPS = {(2, 0): "f3 d n3", (2, 1): "s5 s6 d q3", (2, 2): "d n1 d", (2, 3): "d n2", (3, 0): "f4 s7 d t5", (3, 1): "c5 d q4", (3, 2): "d d", (3, 3): "d t6 c6", (4, 0): "q5 d", (4, 1): "d t7 c7", (4, 2): "d q6", (4, 3): "d d", (5, 0): "d", (5, 2): "d q7", (5, 3): "d", (6, 0): "d d"}
         for m in range(2, ROW_TILES):
-            if m % 2 == 0:
-                for i, a in enumerate(range(m + 1, min(m + 3, FIRST_TURNED))):
-                    xg[a] = transpose_x(xs[a], (2 * i, 2 * i + 1))
-                for a in range(m + 3, min(m + 5, FIRST_TURNED)):
-                    xs[a] = sort_x(a)
-            ahead = m + 1 < ROW_TILES and (m % 2 == 1 or m + 1 >= FIRST_TURNED)
-            if ahead:
-                quantise_x(m + 1, xg[m + 1])
-                xn[m + 1] = negate_x(xg[m + 1])
-            for c in range(CHUNKS):
-                if (m, c) == (ROW_TILES - 1, CHUNKS - 1):
-                    whole_chunk(m, c, 3, 0, Q // 2)
-                    whole_chunk(m, c, 4, Q // 2, Q // 2)
-                else:
-                    whole_chunk(m, c, c if m % 2 == 1 else 4 + c, 0, Q)
-                if m + 1 < ROW_TILES and c == 0 and not ahead:
-                    quantise_x(m + 1, xg[m + 1])
-                    xn[m + 1] = negate_x(xg[m + 1])
-                if m + 1 < ROW_TILES and c == (0 if ahead else 1):
-                    quantise_negated(m + 1, xn[m + 1])
-                for a in range(FIRST_TURNED, ROW_TILES):
-                    if SORT_AT[a] == (m, c):
-                        xs[a] = sort_quartered(a)
-                    if TURN_AT[a] == (m, c):
-                        xg[a] = group_turned(turn_x(xs[a]))
+            for i, c in enumerate((1, 2, 3, 0)):
+                b = next_bank()
+                n = 2 if (m, i) == (ROW_TILES - 1, CHUNKS - 1) else 1
+                for h in range(n):
+                    if h:
+                        b = next_bank()
+                    sums = bank(b, [P, Q // n])
+                    for k, g in enumerate(g_order(c)):
+                        mx_pass(sums, m, g, c, h * Q // n, Q // n, start=(k == 0), stop=(k == CHUNKS - 1))
+                    to_drain.append((sums, m, c, h * Q // n, Q // n))
+                for s in STEPS.get((m, i), "d").split():
+                    step(s)
+        while to_drain:
+            drain()

@@ -15,7 +15,7 @@ B, IN, OUT = 1024, 2048, 2048
 Q = 512
 CHUNKS = 4
 ROW_TILES = B // P
-FIRST_TURNED = 5
+FIRST_TURNED = 4
 NEGATED_TILES = 3
 FLOPS = 2 * B * IN * OUT
 
@@ -44,6 +44,7 @@ def tile_quaternionlinear_kernel(tc, x, Wr, Wi, Wj, Wk, br, bi, bj, bk, out):
         neg_stage = ctx.enter_context(tc.tile_pool(name="neg_stage", bufs=3))
         sort_stage = ctx.enter_context(tc.tile_pool(name="sort_stage", bufs=2))
         turn_stage = ctx.enter_context(tc.tile_pool(name="turn_stage", bufs=3))
+        raw_stage = ctx.enter_context(tc.tile_pool(name="raw_stage", bufs=2))
         out_stage = ctx.enter_context(tc.tile_pool(name="out_stage", bufs=12))
         psum = ctx.enter_context(tc.psum_pool(name="psum", bufs=1))
 
@@ -70,6 +71,7 @@ def tile_quaternionlinear_kernel(tc, x, Wr, Wi, Wj, Wk, br, bi, bj, bk, out):
         wn_scales = keep.tile([P, CHUNKS - 1, Q], U8, align_bytes=256)
 
         nc.gpsimd.memset(bias_rows[:].bitcast(F32), 0.0)
+        nc.vector.memset(idle_values[:].bitcast(F32), 0.0)
         for c in range(CHUNKS):
             for v in range(4):
                 nc.vector.memset(bias_signs[32 * v : 32 * v + 32, c, :], float(BIAS_SIGN[c][v]))
@@ -89,7 +91,7 @@ def tile_quaternionlinear_kernel(tc, x, Wr, Wi, Wj, Wk, br, bi, bj, bk, out):
         x_chunks = x.rearrange("b (g c) -> (b g) c", g=CHUNKS)
 
         def load_x_quartered(m):
-            for a in range(4):
+            for a in (0, 2, 1, 3):
                 nc.sync.dma_start(
                     out=x_rows[32 * a : 32 * a + 32, m, :].rearrange("s (e k) -> s e k", k=P),
                     in_=x_chunks[m * P * CHUNKS : (m + 1) * P * CHUNKS, a * P : (a + 1) * P].rearrange(
@@ -114,7 +116,6 @@ def tile_quaternionlinear_kernel(tc, x, Wr, Wi, Wj, Wk, br, bi, bj, bk, out):
         for m in range(FIRST_TURNED, ROW_TILES):
             load_x_quartered(m)
 
-        nc.gpsimd.memset(idle_values[:].bitcast(F32), 0.0)
         make_identity(nc, identity[:])
 
         def bias_sum(c):
@@ -262,6 +263,17 @@ def tile_quaternionlinear_kernel(tc, x, Wr, Wi, Wj, Wk, br, bi, bj, bk, out):
                 out=out[m * P : (m + 1) * P, c * Q + first : c * Q + first + width], in_=result[:]
             )
 
+        put_by = []
+
+        def put_aside():
+            sums, m, c, first, width = to_drain.pop(0)
+            raw = raw_stage.tile([P, width], F32, name="raw")
+            nc.scalar.copy(out=raw[:], in_=sums[:])
+            put_by.append((raw, m, c, first, width))
+
+        def finish_put_aside():
+            finish(*put_by.pop(0))
+
         open_sums = {}
         passes_done = {}
 
@@ -286,10 +298,10 @@ def tile_quaternionlinear_kernel(tc, x, Wr, Wi, Wj, Wk, br, bi, bj, bk, out):
         wn = {}
 
         def keep_warm(count, b):
+            unread = bank(b, [P, Q])
             for i in range(count):
-                unread = bank(b, [P, Q])
                 nc.tensor.matmul(
-                    out=unread[:], lhsT=idle_values[:, 0:P], rhs=idle_values[:], start=True, stop=True
+                    out=unread[:], lhsT=idle_values[:, 0:P], rhs=idle_values[:], start=(i == 0), stop=(i == count - 1)
                 )
 
         def negw_vector(q):
@@ -304,26 +316,66 @@ def tile_quaternionlinear_kernel(tc, x, Wr, Wi, Wj, Wk, br, bi, bj, bk, out):
         def drain():
             finish(*to_drain.pop(0))
 
-        keep_warm(3, 7)
-        sums = [bias_sum(c) for c in range(CHUNKS)]
-        for c in range(CHUNKS):
-            copy = nc.scalar.copy if c == 0 else nc.vector.tensor_copy
-            copy(out=bias_all[:, c, :], in_=sums[c][:])
+
+        taken = [0]
+
+        def next_bank():
+            taken[0] += 1
+            return (taken[0] - 1) % 8
+
+        def step(s):
+            k, a = s[0], int(s[1:] or 0)
+            if k == "d":
+                drain()
+            if k == "h":
+                put_aside()
+            if k == "z":
+                finish_put_aside()
+            if k == "y":
+                quantise_negated(a, xn[a])
+            if k == "l":
+                load_x_quartered(a)
+            if k == "q":
+                quantise_x(a, xg[a])
+            if k == "n":
+                quantise_negated_weight(a, wn[a])
+            if k == "t":
+                xs[a] = turn_x(xs[a])
+            if k == "c":
+                xg[a] = group_turned(xs[a])
+            if k == "s":
+                xs[a] = sort_quartered(a) if a >= FIRST_TURNED else sort_x(a)
+            if k == "f":
+                xg[a] = transpose_x(xs[a], (next_bank(), next_bank()))
+            if k == "w":
+                wn[a] = negate_weight(a)
+            if k == "v":
+                negw_vector(a)
+        STEPS = {(1, 3): "h s4 h", (2, 0): "f3 d t4", (2, 1): "c4 n3 q3 d", (2, 2): "n1 d s5", (2, 3): "d n2", (3, 0): "q4 s6 d t5 c5", (3, 1): "d", (3, 2): "d t6", (3, 3): "s7 c6 d", (4, 0): "q5 d", (4, 1): "d t7", (4, 2): "d c7", (4, 3): "q6 d", (5, 0): "d", (5, 1): "d", (5, 2): "d q7", (5, 3): "d", (6, 0): "d z", (6, 1): "d z", (0, 0): "s3 v3 v1 d", (0, 1): "y2 d w2", (0, 2): "d", (0, 3): "d"}
+        keep_warm(4, 7)
+        def put_bias(copy, c, sums):
+            copy(out=bias_all[:, c, :], in_=sums[:])
+
+        sums = [bias_sum(c) for c in range(3)]
+        put_bias(nc.vector.tensor_copy, 0, sums[0])
+        put_bias(nc.scalar.copy, 1, sums[1])
+        put_bias(nc.vector.tensor_copy, 2, sums[2])
         xg[0] = new_group()
         transpose_half(word_pairs(0), xg[0], 0, 4)
-        lay_out_scalar(0, 256)
-        lay_out_vector(0, 256)
+        lay_out_scalar(0, 352)
+        lay_out_vector(0, 352)
+        sums.append(bias_sum(3))
         transpose_half(word_pairs(0), xg[0], 1, 5)
+        put_bias(nc.scalar.copy, 3, sums[3])
         keep_warm(2, 0)
         quantise_half(0, xg[0], 0)
         quantise_weight(0)
         quantise_half(0, xg[0], 1)
         xg[1] = transpose_x(word_pairs(1), (6, 7))
-        keep_warm(2, 1)
-        lay_out_scalar(1, 256)
-        lay_out_vector(1, 256)
-        quantise_x(1, xg[1])
         xn[0] = negate_x(xg[0])
+        lay_out_scalar(1, 320)
+        lay_out_vector(1, 320)
+        quantise_x(1, xg[1])
         quantise_weight(1)
         for c in ALL:
             open_sum(0, c, c)
@@ -355,21 +407,13 @@ def tile_quaternionlinear_kernel(tc, x, Wr, Wi, Wj, Wk, br, bi, bj, bk, out):
         xn[2] = negate_x(xg[2])
         quantise_weight(3)
         quantise_x(2, xg[2])
-        xs[3] = sort_x(3)
-        negw_vector(3)
-        negw_vector(1)
-        xs[4] = sort_x(4)
-        wn[2] = negate_weight(2)
         for m in range(2):
             for c in ALL:
                 signed_passes(m, 3, 1, (c,))
                 signed_passes(m, 3, -1, (c,))
                 to_drain.append((open_sums[(m, c)], m, c, 0, Q))
-                if (m, c) == (0, 0):
-                    drain()
-                    quantise_negated(2, xn[2])
-                elif m == 0:
-                    drain()
+                for s in STEPS.get((m, c), "").split():
+                    step(s)
 
         def g_order(c):
             return sorted(range(CHUNKS), key=lambda g: -HAMILTON[g][c][1])
@@ -379,34 +423,6 @@ def tile_quaternionlinear_kernel(tc, x, Wr, Wi, Wj, Wk, br, bi, bj, bk, out):
             for i, g in enumerate(g_order(c)):
                 mx_pass(sums, m, g, c, first, width, start=(i == 0), stop=(i == CHUNKS - 1))
             finish(sums, m, c, first, width)
-
-        taken = [0]
-
-        def next_bank():
-            taken[0] += 1
-            return (taken[0] - 1) % 8
-
-        def step(s):
-            k, a = s[0], int(s[1:] or 0)
-            if k == "d":
-                drain()
-            if k == "q":
-                quantise_x(a, xg[a])
-            if k == "n":
-                quantise_negated_weight(a, wn[a])
-            if k == "t":
-                xs[a] = turn_x(xs[a])
-            if k == "c":
-                xg[a] = group_turned(xs[a])
-            if k == "s":
-                xs[a] = sort_quartered(a) if a >= FIRST_TURNED else sort_x(a)
-            if k == "f":
-                xg[a] = transpose_x(xs[a], (next_bank(), next_bank()))
-            if k == "w":
-                wn[a] = negate_weight(a)
-            if k == "v":
-                negw_vector(a)
-        STEPS = {(2, 0): "f3 d n3", (2, 1): "s5 s6 d q3", (2, 2): "d n1 d", (2, 3): "d n2", (3, 0): "f4 s7 d t5", (3, 1): "c5 d q4", (3, 2): "d d", (3, 3): "d t6 c6", (4, 0): "q5 d", (4, 1): "d t7 c7", (4, 2): "d q6", (4, 3): "d d", (5, 0): "d", (5, 2): "d q7", (5, 3): "d", (6, 0): "d d"}
         for m in range(2, ROW_TILES):
             for i, c in enumerate((1, 2, 3, 0)):
                 b = next_bank()

@@ -44,7 +44,7 @@ def tile_quaternionlinear_kernel(tc, x, Wr, Wi, Wj, Wk, br, bi, bj, bk, out):
         neg_stage = ctx.enter_context(tc.tile_pool(name="neg_stage", bufs=3))
         sort_stage = ctx.enter_context(tc.tile_pool(name="sort_stage", bufs=2))
         turn_stage = ctx.enter_context(tc.tile_pool(name="turn_stage", bufs=3))
-        raw_stage = ctx.enter_context(tc.tile_pool(name="raw_stage", bufs=2))
+        raw_stage = ctx.enter_context(tc.tile_pool(name="raw_stage", bufs=3))
         out_stage = ctx.enter_context(tc.tile_pool(name="out_stage", bufs=12))
         psum = ctx.enter_context(tc.psum_pool(name="psum", bufs=1))
 
@@ -351,7 +351,7 @@ def tile_quaternionlinear_kernel(tc, x, Wr, Wi, Wj, Wk, br, bi, bj, bk, out):
                 wn[a] = negate_weight(a)
             if k == "v":
                 negw_vector(a)
-        STEPS = {(1, 3): "h s4 h", (2, 0): "f3 d t4", (2, 1): "c4 n3 q3 d", (2, 2): "n1 d s5", (2, 3): "d n2", (3, 0): "q4 s6 d t5 c5", (3, 1): "d", (3, 2): "d t6", (3, 3): "s7 c6 d", (4, 0): "q5 d", (4, 1): "d t7", (4, 2): "d c7", (4, 3): "q6 d", (5, 0): "d", (5, 1): "d", (5, 2): "d q7", (5, 3): "d", (6, 0): "d z", (6, 1): "d z", (0, 0): "s3 v3 v1 d", (0, 1): "y2 d w2", (0, 2): "d", (0, 3): "d"}
+        STEPS = {(1, 3): "h s4 h", (2, 0): "f3 d t4", (2, 1): "c4 n3 q3 d", (2, 2): "n1 d s5", (2, 3): "d n2", (3, 0): "q4 s6 d t5 c5", (3, 1): "d", (3, 2): "d t6", (3, 3): "s7 c6 d", (4, 0): "q5 d", (4, 1): "d t7", (4, 2): "d c7 z", (4, 3): "q6 d z", (5, 0): "h z", (5, 1): "d", (5, 2): "h z q7", (5, 3): "d", (6, 0): "h z", (6, 1): "d", (6, 2): "h z", (6, 3): "d", (7, 0): "h z", (7, 1): "d", (7, 2): "h z", (0, 0): "s3 v3 v1 d", (0, 1): "y2 d w2", (0, 2): "d", (0, 3): "d"}
         keep_warm(4, 7)
         def put_bias(copy, c, sums):
             copy(out=bias_all[:, c, :], in_=sums[:])

@@ -44,7 +44,7 @@ def tile_quaternionlinear_kernel(tc, x, Wr, Wi, Wj, Wk, br, bi, bj, bk, out):
         neg_stage = ctx.enter_context(tc.tile_pool(name="neg_stage", bufs=3))
         sort_stage = ctx.enter_context(tc.tile_pool(name="sort_stage", bufs=2))
         turn_stage = ctx.enter_context(tc.tile_pool(name="turn_stage", bufs=3))
-        raw_stage = ctx.enter_context(tc.tile_pool(name="raw_stage", bufs=3))
+        raw_stage = ctx.enter_context(tc.tile_pool(name="raw_stage", bufs=6))
         out_stage = ctx.enter_context(tc.tile_pool(name="out_stage", bufs=12))
         psum = ctx.enter_context(tc.psum_pool(name="psum", bufs=1))
 
@@ -351,7 +351,7 @@ def tile_quaternionlinear_kernel(tc, x, Wr, Wi, Wj, Wk, br, bi, bj, bk, out):
                 wn[a] = negate_weight(a)
             if k == "v":
                 negw_vector(a)
-        STEPS = {(1, 3): "h s4 h", (2, 0): "f3 d t4", (2, 1): "c4 n3 q3 d", (2, 2): "n1 d s5", (2, 3): "d n2", (3, 0): "q4 s6 d t5 c5", (3, 1): "d", (3, 2): "d t6", (3, 3): "s7 c6 d", (4, 0): "q5 d", (4, 1): "d t7", (4, 2): "d c7 z", (4, 3): "q6 d z", (5, 0): "h z", (5, 1): "d", (5, 2): "h z q7", (5, 3): "d", (6, 0): "h z", (6, 1): "d", (6, 2): "h z", (6, 3): "d", (7, 0): "h z", (7, 1): "d", (7, 2): "h z", (0, 0): "s3 v3 v1 d", (0, 1): "y2 d w2", (0, 2): "d", (0, 3): "d"}
+        STEPS = {(1, 3): "h s4 h", (2, 0): "f3 d t4", (2, 1): "c4 n3 q3 d", (2, 2): "n1 d s5", (2, 3): "d n2", (3, 0): "q4 s6 h h t5 c5", (3, 1): "d", (3, 2): "d t6", (3, 3): "s7 c6 d", (4, 0): "q5 d", (4, 1): "d t7", (4, 2): "d c7 z z", (4, 3): "q6 d z", (5, 0): "h z z", (5, 1): "d z", (5, 2): "h z q7", (5, 3): "d", (6, 0): "h z", (6, 1): "d", (6, 2): "h z", (6, 3): "d", (7, 0): "h z", (7, 1): "d", (7, 2): "d d", (0, 0): "s3 v3 v1 d", (0, 1): "y2 d w2", (0, 2): "h", (0, 3): "d"}
         keep_warm(4, 7)
         def put_bias(copy, c, sums):
             copy(out=bias_all[:, c, :], in_=sums[:])

@@ -16,7 +16,7 @@ Q = 512
 CHUNKS = 4
 ROW_TILES = B // P
 FIRST_TURNED = 4
-NEGATED_TILES = 3
+NEGATED_TILES = 2
 FLOPS = 2 * B * IN * OUT
 
 HAMILTON = (
@@ -100,7 +100,8 @@ def tile_quaternionlinear_kernel(tc, x, Wr, Wi, Wj, Wk, br, bi, bj, bk, out):
                 )
 
         for v in range(4):
-            nc.sync.dma_start(
+            queue = nc.sync if v % 2 == 0 else nc.scalar
+            queue.dma_start(
                 out=bias_rows[32 * v : 32 * v + 1, :], in_=biases[v].rearrange("(o n) -> o n", o=1)
             )
         load_x_half(0, 0)
@@ -351,7 +352,7 @@ def tile_quaternionlinear_kernel(tc, x, Wr, Wi, Wj, Wk, br, bi, bj, bk, out):
                 wn[a] = negate_weight(a)
             if k == "v":
                 negw_vector(a)
-        STEPS = {(1, 3): "h s4 h", (2, 0): "f3 d t4", (2, 1): "c4 n3 q3 d", (2, 2): "n1 d s5", (2, 3): "d n2", (3, 0): "q4 s6 h h t5 c5", (3, 1): "d", (3, 2): "d t6", (3, 3): "s7 c6 d", (4, 0): "q5 d", (4, 1): "d t7", (4, 2): "d c7 z z", (4, 3): "q6 d z", (5, 0): "h z z", (5, 1): "d z", (5, 2): "h z q7", (5, 3): "d", (6, 0): "h z", (6, 1): "d", (6, 2): "h z", (6, 3): "d", (7, 0): "h z", (7, 1): "d", (7, 2): "d d", (0, 0): "s3 v3 v1 d", (0, 1): "y2 d w2", (0, 2): "h", (0, 3): "d"}
+        STEPS = {(1, 3): "s4 d", (2, 0): "f3 d t4", (2, 1): "h c4 q3 d", (2, 2): "z s5 d", (2, 3): "z", (3, 0): "q4 s6 h h t5 c5", (3, 1): "d", (3, 2): "d t6 z", (3, 3): "s7 c6 d", (4, 0): "q5 d z", (4, 1): "d t7", (4, 2): "d c7 z", (4, 3): "q6 d z", (5, 0): "h z", (5, 1): "d z", (5, 2): "h z q7", (5, 3): "d", (6, 0): "h z", (6, 1): "d", (6, 2): "h z", (6, 3): "d", (7, 0): "h z", (7, 1): "d", (7, 2): "d d", (0, 0): "s3 q2 v3 h", (0, 1): "h v1 n3", (0, 2): "h v2 n1", (0, 3): "h n2"}
         keep_warm(4, 7)
         def put_bias(copy, c, sums):
             copy(out=bias_all[:, c, :], in_=sums[:])
@@ -373,15 +374,15 @@ def tile_quaternionlinear_kernel(tc, x, Wr, Wi, Wj, Wk, br, bi, bj, bk, out):
         quantise_half(0, xg[0], 1)
         xg[1] = transpose_x(word_pairs(1), (6, 7))
         xn[0] = negate_x(xg[0])
-        lay_out_scalar(1, 320)
-        lay_out_vector(1, 320)
+        lay_out_scalar(1, 352)
+        lay_out_vector(1, 352)
         quantise_x(1, xg[1])
         quantise_weight(1)
         for c in ALL:
             open_sum(0, c, c)
         signed_passes(0, 0, 1, ALL)
         xg[2] = transpose_x(word_pairs(2), (4, 5))
-        lay_out_scalar(2, 256)
+        lay_out_scalar(2, 288)
         quantise_negated(0, xn[0])
         open_sum(1, 2, 6)
         open_sum(1, 3, 7)
@@ -393,7 +394,7 @@ def tile_quaternionlinear_kernel(tc, x, Wr, Wi, Wj, Wk, br, bi, bj, bk, out):
         open_sum(1, 1, 5)
         signed_passes(1, 0, 1, (0, 1))
         signed_passes(1, 1, 1, (0, 1))
-        lay_out_vector(2, 256)
+        lay_out_vector(2, 288)
         xn[1] = negate_x(xg[1])
         quantise_weight(2)
         signed_passes(0, 2, 1, ALL)
@@ -402,11 +403,9 @@ def tile_quaternionlinear_kernel(tc, x, Wr, Wi, Wj, Wk, br, bi, bj, bk, out):
         quantise_negated(1, xn[1])
         signed_passes(1, 1, -1, ALL)
         signed_passes(1, 2, -1, ALL)
-        lay_out_vector(3, 128)
-        lay_out_scalar(3, 128)
-        xn[2] = negate_x(xg[2])
+        lay_out_vector(3, 192)
+        lay_out_scalar(3, 192)
         quantise_weight(3)
-        quantise_x(2, xg[2])
         for m in range(2):
             for c in ALL:
                 signed_passes(m, 3, 1, (c,))

from contextlib import ExitStack

import concourse.mybir as mybir
from concourse.masks import make_identity

F32 = mybir.dt.float32
BF16 = mybir.dt.bfloat16
U32 = mybir.dt.uint32
U8 = mybir.dt.uint8
FP8X4 = mybir.dt.float8_e4m3fn_x4

P = 128
PACK = 4
B, IN, OUT = 1024, 2048, 2048
Q = 512
CHUNKS = 4
ROW_TILES = B // P
FIRST_TURNED = 4
NEGATED_TILES = 2
FLOPS = 2 * B * IN * OUT

HAMILTON = (
    ((0, 1), (1, 1), (2, 1), (3, 1)),
    ((1, -1), (0, 1), (3, 1), (2, -1)),
    ((2, -1), (3, -1), (0, 1), (1, 1)),
    ((3, -1), (2, 1), (1, -1), (0, 1)),
)
BIAS_SIGN = (
    (1, -1, -1, -1),
    (1, 1, 1, -1),
    (1, -1, 1, 1),
    (1, 1, -1, 1),
)


def tile_quaternionlinear_kernel(tc, x, Wr, Wi, Wj, Wk, br, bi, bj, bk, out):
    nc = tc.nc
    weights = (Wr, Wi, Wj, Wk)
    biases = (br, bi, bj, bk)

    with ExitStack() as ctx:
        keep = ctx.enter_context(tc.tile_pool(name="keep", bufs=1))
        x_stage = ctx.enter_context(tc.tile_pool(name="x_stage", bufs=5))
        neg_stage = ctx.enter_context(tc.tile_pool(name="neg_stage", bufs=3))
        sort_stage = ctx.enter_context(tc.tile_pool(name="sort_stage", bufs=2))
        turn_stage = ctx.enter_context(tc.tile_pool(name="turn_stage", bufs=3))
        raw_stage = ctx.enter_context(tc.tile_pool(name="raw_stage", bufs=6))
        out_stage = ctx.enter_context(tc.tile_pool(name="out_stage", bufs=12))
        psum = ctx.enter_context(tc.psum_pool(name="psum", bufs=1))

        ctx.enter_context(tc.manual_schedule())

        def bank(b, shape):
            return psum.tile(shape, F32, name="bank%d" % b, tag="bank%d" % b)

        identity = keep.tile([P, P], F32)
        bias_rows = keep.tile([P, Q], BF16)
        idle_values = keep.tile([P, Q], BF16)
        bias_signs = keep.tile([P, CHUNKS, P], BF16)
        bias_all = keep.tile([P, CHUNKS, Q], F32)
        x_rows = keep.tile([P, ROW_TILES, IN], BF16)
        x_codes = keep.tile([P, ROW_TILES, CHUNKS * P], U32, align_bytes=256)
        x_scales = keep.tile([P, ROW_TILES, CHUNKS * P], U8, align_bytes=256)
        xn_codes = keep.tile([P, NEGATED_TILES, (CHUNKS - 1) * P], U32, align_bytes=256)
        xn_scales = keep.tile([P, NEGATED_TILES, (CHUNKS - 1) * P], U8, align_bytes=256)
        w_rows = keep.tile([P, CHUNKS, PACK, Q], BF16)
        w_grouped = keep.tile([P, CHUNKS, Q, PACK], BF16, align_bytes=64)
        w_codes = keep.tile([P, CHUNKS, Q], U32, align_bytes=256)
        w_scales = keep.tile([P, CHUNKS, Q], U8, align_bytes=256)
        wn_codes = keep.tile([P, CHUNKS - 1, Q], U32, align_bytes=256)
        wn_scales = keep.tile([P, CHUNKS - 1, Q], U8, align_bytes=256)

        nc.gpsimd.memset(bias_rows[:].bitcast(F32), 0.0)
        nc.vector.memset(idle_values[:].bitcast(F32), 0.0)
        for c in range(CHUNKS):
            for v in range(4):
                nc.vector.memset(bias_signs[32 * v : 32 * v + 32, c, :], float(BIAS_SIGN[c][v]))

        def load_weight(q):
            nc.sync.dma_start(
                out=w_rows[:, q, :, :], in_=weights[q].rearrange("(p t) n -> p t n", t=PACK)
            )

        def load_x(m):
            nc.sync.dma_start(out=x_rows[:, m, :], in_=x[m * P : (m + 1) * P, :])

        def load_x_half(m, h):
            cols = slice(h * IN // 2, (h + 1) * IN // 2)
            nc.sync.dma_start(out=x_rows[:, m, cols], in_=x[m * P : (m + 1) * P, cols])

        x_chunks = x.rearrange("b (g c) -> (b g) c", g=CHUNKS)

        def load_x_quartered(m):
            for a in (0, 2, 1, 3):
                nc.sync.dma_start(
                    out=x_rows[32 * a : 32 * a + 32, m, :].rearrange("s (e k) -> s e k", k=P),
                    in_=x_chunks[m * P * CHUNKS : (m + 1) * P * CHUNKS, a * P : (a + 1) * P].rearrange(
                        "(s e) k -> s e k", e=4 * CHUNKS
                    ),
                )

        for v in range(4):
            queue = nc.sync if v % 2 == 0 else nc.scalar
            queue.dma_start(
                out=bias_rows[32 * v : 32 * v + 1, :], in_=biases[v].rearrange("(o n) -> o n", o=1)
            )
        load_x_half(0, 0)
        load_weight(0)
        load_x_half(0, 1)
        load_x(1)
        load_weight(1)
        load_x(2)
        load_weight(2)
        load_weight(3)
        for m in range(3, FIRST_TURNED):
            load_x(m)
        for m in range(FIRST_TURNED, ROW_TILES):
            load_x_quartered(m)

        make_identity(nc, identity[:])

        def bias_sum(c):
            sums = bank(c, [P, Q])
            nc.tensor.matmul(
                out=sums[:], lhsT=bias_signs[:, c, :], rhs=bias_rows[:], start=True, stop=True
            )
            return sums

        def lay_out(q, copy, cols):
            copy(
                out=w_grouped[:, q, cols, :].rearrange("p (c i) t -> p c t i", i=4),
                in_=w_rows[:, q, :, cols].rearrange("p t (c i) -> p c t i", i=4),
            )

        def lay_out_vector(q, n):
            lay_out(q, nc.vector.tensor_copy, slice(0, n))

        def lay_out_scalar(q, n):
            lay_out(q, nc.scalar.copy, slice(n, Q))

        def quantise_weight(q):
            nc.vector.quantize_mx(
                out=w_codes[:, q, :].bitcast(FP8X4),
                scales=w_scales[:, q, :],
                in_=w_grouped[:, q, :, :].rearrange("p n t -> p (n t)"),
            )

        def negate_weight(q):
            negated = neg_stage.tile([P, Q * PACK], BF16, align_bytes=64, name="w_negated")
            nc.scalar.mul(negated[:], w_grouped[:, q, :, :].rearrange("p n t -> p (n t)"), -1.0)
            return negated

        def quantise_negated_weight(q, negated):
            nc.vector.quantize_mx(
                out=wn_codes[:, q - 1, :].bitcast(FP8X4), scales=wn_scales[:, q - 1, :], in_=negated[:]
            )

        def word_pairs(m):
            return x_rows[:, m, :].bitcast(F32).rearrange("p (g j u) -> p g u j", g=CHUNKS, u=2)

        def sort_x(m):
            sorted_words = sort_stage.tile([P, CHUNKS, 2, P], F32, name="sorted_words")
            nc.scalar.copy(out=sorted_words[:], in_=word_pairs(m))
            return sorted_words[:]

        def sort_quartered(m):
            sorted_words = turn_stage.tile([P, 4 * CHUNKS, 2, 32], F32, align_bytes=64, name="sorted_quarters")
            nc.scalar.copy(
                out=sorted_words[:],
                in_=x_rows[:, m, :].bitcast(F32).rearrange("p (e j u) -> p e u j", j=32, u=2),
            )
            return sorted_words

        def turn_x(sorted_words):
            turned = turn_stage.tile([P, 4, CHUNKS, 2, 32], F32, align_bytes=64, name="turned")
            nc.vector.transpose(
                out=turned[:].rearrange("p r g u s -> p (r g u s)"),
                in_=sorted_words[:].rearrange("p e u j -> p (e u j)"),
            )
            return turned

        def group_turned(turned):
            grouped = x_stage.tile([P, CHUNKS * P * PACK], BF16, align_bytes=64, name="x_grouped")
            grouped_words = grouped[:].bitcast(F32).rearrange("p (g s r u) -> p g s r u", g=CHUNKS, r=4, u=2)
            for g in range(CHUNKS):
                nc.scalar.copy(
                    out=grouped_words[:, g, :, :, :], in_=turned[:, :, g, :, :].rearrange("p r u s -> p s r u")
                )
            return grouped

        def new_group():
            return x_stage.tile([P, CHUNKS * P * PACK], BF16, align_bytes=64, name="x_grouped")

        def transpose_half(words, grouped, h, b):
            grouped_words = grouped[:].bitcast(F32).rearrange("p (g r u) -> p g r u", g=CHUNKS, u=2)
            flipped = bank(b, [P, 2, 2, P])
            for gi in range(2):
                for u in range(2):
                    nc.tensor.transpose(flipped[:, gi, u, :], words[:, 2 * h + gi, u, :], identity[:])
            nc.scalar.copy(
                out=grouped_words[:, 2 * h : 2 * h + 2, :, :],
                in_=flipped[:].rearrange("p g u r -> p g r u"),
            )

        def transpose_x(words, banks):
            grouped = new_group()
            for h in range(2):
                transpose_half(words, grouped, h, banks[h])
            return grouped

        def quantise_half(m, grouped, h):
            words = slice(2 * h * P, 2 * (h + 1) * P)
            nc.vector.quantize_mx(
                out=x_codes[:, m, words].bitcast(FP8X4),
                scales=x_scales[:, m, words],
                in_=grouped[:, 2 * h * P * PACK : 2 * (h + 1) * P * PACK],
            )

        def quantise_x(m, grouped):
            nc.vector.quantize_mx(
                out=x_codes[:, m, :].bitcast(FP8X4), scales=x_scales[:, m, :], in_=grouped[:]
            )

        def negate_x(grouped):
            negated = neg_stage.tile([P, (CHUNKS - 1) * P * PACK], BF16, align_bytes=64, name="x_negated")
            nc.vector.tensor_scalar_mul(out=negated[:], in0=grouped[:, P * PACK :], scalar1=-1.0)
            return negated

        def quantise_negated(m, negated):
            for words, values in (
                (slice(0, 2 * P), slice(0, 2 * P * PACK)),
                (slice(2 * P, 3 * P), slice(2 * P * PACK, 3 * P * PACK)),
            ):
                nc.vector.quantize_mx(
                    out=xn_codes[:, m, words].bitcast(FP8X4), scales=xn_scales[:, m, words], in_=negated[:, values]
                )

        def mx_pass(sums, m, g, c, first, width, start, stop):
            cols = slice(first, first + width)
            q, sign = HAMILTON[g][c]
            stationary = (x_codes[:, m, g * P : (g + 1) * P], x_scales[:, m, g * P : (g + 1) * P])
            moving = (w_codes[:, q, cols], w_scales[:, q, cols])
            if sign < 0 and m < NEGATED_TILES:
                rows = slice((g - 1) * P, g * P)
                stationary = (xn_codes[:, m, rows], xn_scales[:, m, rows])
            elif sign < 0:
                moving = (wn_codes[:, q - 1, cols], wn_scales[:, q - 1, cols])
            nc.tensor.matmul_mx(
                out=sums[:],
                lhsT=stationary[0].bitcast(FP8X4),
                lhsT_scale=stationary[1],
                rhs=moving[0].bitcast(FP8X4),
                rhs_scale=moving[1],
                start=start,
                stop=stop,
            )

        def finish(sums, m, c, first, width):
            result = out_stage.tile([P, width], F32, name="result")
            nc.vector.tensor_tensor(
                out=result[:], in0=sums[:], in1=bias_all[:, c, first : first + width], op=mybir.AluOpType.add
            )
            nc.sync.dma_start(
                out=out[m * P : (m + 1) * P, c * Q + first : c * Q + first + width], in_=result[:]
            )

        put_by = []

        def put_aside():
            sums, m, c, first, width = to_drain.pop(0)
            raw = raw_stage.tile([P, width], F32, name="raw")
            nc.scalar.copy(out=raw[:], in_=sums[:])
            put_by.append((raw, m, c, first, width))

        def finish_put_aside():
            finish(*put_by.pop(0))

        open_sums = {}
        passes_done = {}

        def open_sum(m, c, b):
            open_sums[(m, c)] = bank(b, [P, Q])
            passes_done[(m, c)] = 0

        def signed_passes(m, q, sign, chunks):
            for c in chunks:
                for g in range(CHUNKS):
                    if HAMILTON[g][c] == (q, sign):
                        passes_done[(m, c)] += 1
                        mx_pass(
                            open_sums[(m, c)], m, g, c, 0, Q,
                            start=(passes_done[(m, c)] == 1), stop=(passes_done[(m, c)] == CHUNKS),
                        )

        ALL = range(CHUNKS)
        xg = {}
        xn = {}
        xs = {}
        wn = {}

        def keep_warm(count, b):
            unread = bank(b, [P, Q])
            for i in range(count):
                nc.tensor.matmul(
                    out=unread[:], lhsT=idle_values[:, 0:P], rhs=idle_values[:], start=(i == 0), stop=(i == count - 1)
                )

        def negw_vector(q):
            negated = neg_stage.tile([P, Q * PACK], BF16, align_bytes=64, name="w_negated")
            nc.vector.tensor_scalar_mul(
                out=negated[:], in0=w_grouped[:, q, :, :].rearrange("p n t -> p (n t)"), scalar1=-1.0
            )
            wn[q] = negated

        to_drain = []

        def drain():
            finish(*to_drain.pop(0))


        taken = [0]

        def next_bank():
            taken[0] += 1
            return (taken[0] - 1) % 8

        def step(s):
            k, a = s[0], int(s[1:] or 0)
            if k == "d":
                drain()
            if k == "h":
                put_aside()
            if k == "z":
                finish_put_aside()
            if k == "y":
                quantise_negated(a, xn[a])
            if k == "l":
                load_x_quartered(a)
            if k == "q":
                quantise_x(a, xg[a])
            if k == "n":
                quantise_negated_weight(a, wn[a])
            if k == "t":
                xs[a] = turn_x(xs[a])
            if k == "c":
                xg[a] = group_turned(xs[a])
            if k == "s":
                xs[a] = sort_quartered(a) if a >= FIRST_TURNED else sort_x(a)
            if k == "f":
                xg[a] = transpose_x(xs[a], (next_bank(), next_bank()))
            if k == "w":
                wn[a] = negate_weight(a)
            if k == "v":
                negw_vector(a)
        STEPS = {(1, 3): "s4 d", (2, 0): "f3 d t4", (2, 1): "h c4 q3 d", (2, 2): "z s5 d", (2, 3): "z", (3, 0): "q4 s6 h h t5 c5", (3, 1): "d", (3, 2): "d t6 z", (3, 3): "s7 c6 d", (4, 0): "q5 d z", (4, 1): "d t7", (4, 2): "d c7 z", (4, 3): "q6 d z", (5, 0): "h z", (5, 1): "d z", (5, 2): "h z q7", (5, 3): "d", (6, 0): "h z", (6, 1): "d", (6, 2): "h z", (6, 3): "d", (7, 0): "h z", (7, 1): "d", (7, 2): "d d", (0, 0): "s3 q2 v3 h", (0, 1): "h v1 n3", (0, 2): "h v2 n1", (0, 3): "h n2"}
        keep_warm(4, 7)
        def put_bias(copy, c, sums):
            copy(out=bias_all[:, c, :], in_=sums[:])

        sums = [bias_sum(c) for c in range(3)]
        put_bias(nc.vector.tensor_copy, 0, sums[0])
        put_bias(nc.scalar.copy, 1, sums[1])
        put_bias(nc.vector.tensor_copy, 2, sums[2])
        xg[0] = new_group()
        transpose_half(word_pairs(0), xg[0], 0, 4)
        lay_out_scalar(0, 352)
        lay_out_vector(0, 352)
        sums.append(bias_sum(3))
        transpose_half(word_pairs(0), xg[0], 1, 5)
        put_bias(nc.scalar.copy, 3, sums[3])
        keep_warm(2, 0)
        quantise_half(0, xg[0], 0)
        quantise_weight(0)
        quantise_half(0, xg[0], 1)
        xg[1] = transpose_x(word_pairs(1), (6, 7))
        xn[0] = negate_x(xg[0])
        lay_out_scalar(1, 352)
        lay_out_vector(1, 352)
        quantise_x(1, xg[1])
        quantise_weight(1)
        for c in ALL:
            open_sum(0, c, c)
        signed_passes(0, 0, 1, ALL)
        xg[2] = transpose_x(word_pairs(2), (4, 5))
        lay_out_scalar(2, 288)
        quantise_negated(0, xn[0])
        open_sum(1, 2, 6)
        open_sum(1, 3, 7)
        signed_passes(1, 0, 1, (2, 3))
        signed_passes(0, 1, 1, ALL)
        signed_passes(1, 1, 1, (2, 3))
        signed_passes(0, 1, -1, ALL)
        open_sum(1, 0, 4)
        open_sum(1, 1, 5)
        signed_passes(1, 0, 1, (0, 1))
        signed_passes(1, 1, 1, (0, 1))
        lay_out_vector(2, 288)
        xn[1] = negate_x(xg[1])
        quantise_weight(2)
        signed_passes(0, 2, 1, ALL)
        signed_passes(0, 2, -1, ALL)
        signed_passes(1, 2, 1, ALL)
        quantise_negated(1, xn[1])
        signed_passes(1, 1, -1, ALL)
        signed_passes(1, 2, -1, ALL)
        lay_out_vector(3, 192)
        lay_out_scalar(3, 192)
        quantise_weight(3)
        for m in range(2):
            for c in ALL:
                signed_passes(m, 3, 1, (c,))
                signed_passes(m, 3, -1, (c,))
                to_drain.append((open_sums[(m, c)], m, c, 0, Q))
                for s in STEPS.get((m, c), "").split():
                    step(s)

        def g_order(c):
            return sorted(range(CHUNKS), key=lambda g: -HAMILTON[g][c][1])

        def whole_chunk(m, c, b, first, width):
            sums = bank(b, [P, width])
            for i, g in enumerate(g_order(c)):
                mx_pass(sums, m, g, c, first, width, start=(i == 0), stop=(i == CHUNKS - 1))
            finish(sums, m, c, first, width)
        for m in range(2, ROW_TILES):
            for i, c in enumerate((1, 2, 3, 0)):
                b = next_bank()
                n = 2 if (m, i) == (ROW_TILES - 1, CHUNKS - 1) else 1
                for h in range(n):
                    if h:
                        b = next_bank()
                    sums = bank(b, [P, Q // n])
                    for k, g in enumerate(g_order(c)):
                        mx_pass(sums, m, g, c, h * Q // n, Q // n, start=(k == 0), stop=(k == CHUNKS - 1))
                    to_drain.append((sums, m, c, h * Q // n, Q // n))
                for s in STEPS.get((m, i), "d").split():
                    step(s)
        while to_drain:
            drain()
